import numpy as np
import ml_dtypes


def mxq(x, axis, fmt="e4m3"):
    dtype, down = {"e4m3": (ml_dtypes.float8_e4m3fn, 7), "e5m2": (ml_dtypes.float8_e5m2, 14)}[fmt]
    v = np.moveaxis(np.asarray(x, np.float32).astype(ml_dtypes.bfloat16).astype(np.float64), axis, -1)
    blocks = v.reshape(v.shape[:-1] + (-1, 32))
    amax = np.abs(blocks).max(-1, keepdims=True)
    byte = np.maximum(np.where(amax > 0, np.frexp(amax)[1] - 1 + 127, 0) - down, 1)
    scale = np.exp2(byte - 127.0)
    codes = (blocks / scale).astype(np.float32).astype(dtype).astype(np.float64)
    return np.moveaxis((codes * scale).reshape(v.shape), -1, axis)


WIDE = False


def mx_kscale(k):
    if not WIDE:
        return np.ones(k)
    levels = np.array([10, -10, 5, -5, 0])
    a = np.random.permutation(np.resize(levels, k // 512 * 4)).reshape(k // 512, 4)
    idx = np.arange(k)
    return np.exp2(a[idx // 512, idx % 128 // 32])


BF16 = ml_dtypes.bfloat16


def bf(x):
    return np.asarray(x, np.float32).astype(BF16)


def f64(x):
    return np.asarray(x).astype(np.float64)


B, C, T, H = 4, 512, 256, 8192
EPS_LN = 1e-5
EPS_STD = 1e-5


def ln_dim1(z, g, b):
    mu = z.mean(axis=1, keepdims=True)
    var = ((z - mu) ** 2).mean(axis=1, keepdims=True)
    return (z - mu) / np.sqrt(var + EPS_LN) * g[None, :, None] + b[None, :, None]


def stats(x, m):
    mean = (m * x).sum(axis=2)
    std = np.sqrt(np.maximum((m * x * x).sum(axis=2) - mean ** 2, EPS_STD))
    return mean, std


def setup_inputs():
    s = mx_kscale(H)
    drop = np.random.randint(B, size=T)
    mask = (np.arange(B)[:, None, None] != drop[None, None, :]) * 1.0
    off = 0.5 * np.random.standard_normal((B, C, 1))
    gain = 0.5 + np.random.random((B, C, 1))
    pad = np.random.standard_normal((B, C, 1)) * (1.0 - mask)
    x = off + gain * np.random.standard_normal((B, C, T)) + pad
    return {"h": bf(np.tanh(np.random.standard_normal((B, H, T))) * s[None, :, None]),
            "x": bf(x),
            "mask": bf(mask),
            "w2": bf(np.random.standard_normal((C, H)) * 3.0 / np.sqrt(H) / s[None, :]),
            "b2": bf(0.1 * np.random.standard_normal(C)),
            "g2": bf(1.0 + 0.1 * np.random.standard_normal(2 * C)),
            "be2": bf(0.1 * np.random.standard_normal(2 * C))}


def reference(h, x, mask, w2, b2, g2, be2):
    x, mask = f64(x), f64(mask)
    alpha = (mxq(f64(w2), 1, "e4m3") @ mxq(f64(h), 1, "e4m3")) + f64(b2)[None, :, None]
    alpha = np.where(mask == 0, -np.inf, alpha)
    e = np.exp(alpha - alpha.max(axis=2, keepdims=True))
    alpha = e / e.sum(axis=2, keepdims=True)
    mean, std = stats(x, alpha)
    out = np.concatenate([mean, std], axis=1)[:, :, None]
    return ln_dim1(out, f64(g2), f64(be2))

@@ -1,0 +1,333 @@
+from contextlib import ExitStack
+
+import concourse.mybir as mybir
+from concourse.masks import make_identity
+
+F32 = mybir.dt.float32
+BF16 = mybir.dt.bfloat16
+U32 = mybir.dt.uint32
+U8 = mybir.dt.uint8
+FP8X4 = mybir.dt.float8_e4m3fn_x4
+ALU = mybir.AluOpType
+ACT = mybir.ActivationFunctionType
+AXIS = mybir.AxisListType
+
+B, C, T, H = 4, 512, 256, 8192
+EPS_LN = 1e-5
+EPS_STD = 1e-5
+
+P = 128
+PACK = 4
+K_PASS = P * PACK
+PASSES = H // K_PASS
+C_TILES = C // P
+CHUNK = 4
+CHUNKS = PASSES // CHUNK
+K_CHUNK = CHUNK * K_PASS
+BANK = 512
+ROWS = 2 * C_TILES
+
+VECTOR_FRAMES = 112
+RUN = 4
+AHEAD = 3
+MASKED = 1.0e30
+
+FLOPS = 2 * B * C * H * T
+
+
+def tile_attentivestatspool_pb_k_kernel(tc, h, x, mask, w2, b2, g2, be2, out):
+    nc = tc.nc
+    with ExitStack() as ctx:
+        keep = ctx.enter_context(tc.tile_pool(name="keep", bufs=1))
+        raw = ctx.enter_context(tc.tile_pool(name="raw", bufs=AHEAD))
+        grouped = ctx.enter_context(tc.tile_pool(name="grouped", bufs=3))
+        frames = ctx.enter_context(tc.tile_pool(name="frames", bufs=C_TILES))
+        psum = ctx.enter_context(tc.psum_pool(name="psum", bufs=8))
+        small = ctx.enter_context(tc.tile_pool(name="small", bufs=1))
+        ctx.enter_context(tc.manual_schedule())
+
+        w_codes = keep.tile([P, C_TILES, PASSES, P], U32, align_bytes=64)
+        w_scales = keep.tile([P, C_TILES, PASSES, P], U8, align_bytes=64)
+        h_codes = keep.tile([P, B, PASSES, T], U32, align_bytes=64)
+        h_scales = keep.tile([P, B, PASSES, T], U8, align_bytes=64)
+        x_sb = keep.tile([P, B, C_TILES, T], BF16)
+        masked_add = keep.tile([P, B, T], F32)
+        neg_max = keep.tile([P, B, C_TILES], F32)
+        sum_e = keep.tile([P, B, C_TILES], F32)
+        sum_ex = keep.tile([P, B, C_TILES], F32)
+        sum_exx = keep.tile([P, B, C_TILES], F32)
+
+        identity = keep.tile([P, P], F32)
+        make_identity(nc, identity[:])
+        mask_rows = keep.tile([P, B * T], BF16)
+        nc.vector.memset(mask_rows[:], 0.0)
+        nc.scalar.dma_start(out=mask_rows[0:1, :], in_=mask.rearrange("b o t -> o (b t)"))
+        ones = keep.tile([P, P], BF16)
+        nc.vector.memset(ones[:], 1.0)
+        averager = keep.tile([P, P], F32)
+        nc.vector.memset(averager[:], 1.0 / (2 * C))
+        one_column = keep.tile([P, 1], F32)
+        nc.vector.memset(one_column[:], 1.0)
+        normed = keep.tile([P, P], F32)
+        nc.vector.memset(normed[:], 0.0)
+
+        table_warmer = keep.tile([P, 1], F32)
+        nc.scalar.activation(out=table_warmer[:], in_=one_column[:], func=ACT.Exp)
+
+        masked_add_flat = masked_add[:].rearrange("p b t -> p (b t)")
+        for half in range(B * T // BANK):
+            cols = slice(half * BANK, (half + 1) * BANK)
+            mask_everywhere = psum.tile([P, BANK], F32, tag="bank")
+            nc.tensor.matmul(
+                out=mask_everywhere[:], lhsT=ones[:], rhs=mask_rows[:, cols], start=True, stop=True
+            )
+            nc.vector.tensor_scalar(
+                out=masked_add_flat[:, cols],
+                in0=mask_everywhere[:],
+                scalar1=0.0,
+                scalar2=MASKED,
+                op0=ALU.is_equal,
+                op1=ALU.mult,
+            )
+
+        stream = []
+        for i in range(B):
+            stream.extend([("w", i, kc) for kc in range(CHUNKS)])
+            stream.extend([("h", i, kc) for kc in range(CHUNKS)])
+        n_chunks = len(stream)
+
+        raw_tiles = {}
+        grouped_tiles = {}
+        logits = {}
+        e_tiles = {}
+
+        def units_of(kind, i):
+            if kind == "w":
+                return [(i, b) for b in range(i)]
+            return [(ct, i) for ct in range(i + 1)]
+
+        def load(n):
+            kind, i, kc = stream[n]
+            k_rows = slice(kc * K_CHUNK, (kc + 1) * K_CHUNK)
+            if kind == "w":
+                w_raw = raw.tile([P, K_CHUNK], BF16, tag="w_raw")
+                nc.sync.dma_start(out=w_raw[:], in_=w2[i * P : (i + 1) * P, k_rows])
+                raw_tiles[n] = w_raw
+            else:
+                if kc == 0:
+                    nc.sync.dma_start(
+                        out=x_sb[:, i, :, :], in_=x[i].rearrange("(ct p) t -> p ct t", p=P)
+                    )
+                h_raw = raw.tile([P, CHUNK, PACK, T], BF16, tag="h_raw")
+                nc.sync.dma_start(
+                    out=h_raw[:],
+                    in_=h[i, k_rows, :].rearrange("(g p j) t -> p g j t", p=P, j=PACK),
+                )
+                raw_tiles[n] = h_raw
+
+        def group(n):
+            kind, i, kc = stream[n]
+            if kind == "w":
+                w_grouped = grouped.tile([P, CHUNK, P, PACK], BF16, tag="w_grouped", align_bytes=64)
+                words = raw_tiles[n][:].bitcast(F32).rearrange("c (g q u) -> c g u q", g=CHUNK, u=2)
+                grouped_words = w_grouped[:].bitcast(F32)
+                for pair in range(CHUNK // 2):
+                    transposed = psum.tile([P, 2, 2, P], F32, tag="bank")
+                    for g in range(2):
+                        for u in range(2):
+                            nc.tensor.transpose(
+                                transposed[:, g, u, :], words[:, 2 * pair + g, u, :], identity[:]
+                            )
+                    nc.scalar.copy(
+                        out=grouped_words[:, 2 * pair : 2 * pair + 2, :, :],
+                        in_=transposed[:].rearrange("q g u c -> q g c u"),
+                    )
+                grouped_tiles[n] = w_grouped
+            else:
+                h_grouped = grouped.tile([P, CHUNK, T, PACK], BF16, tag="h_grouped", align_bytes=64)
+                src = raw_tiles[n][:].rearrange("p g j (c r) -> p g c j r", r=RUN)
+                dst = h_grouped[:].rearrange("p g (c r) j -> p g c j r", r=RUN)
+                split = VECTOR_FRAMES // RUN
+                nc.vector.tensor_copy(out=dst[:, :, 0:split], in_=src[:, :, 0:split])
+                for g in range(CHUNK):
+                    nc.scalar.copy(out=dst[:, g, split:], in_=src[:, g, split:])
+                grouped_tiles[n] = h_grouped
+
+        def quantise(n):
+            kind, i, kc = stream[n]
+            passes = slice(kc * CHUNK, (kc + 1) * CHUNK)
+            codes, scales = (w_codes, w_scales) if kind == "w" else (h_codes, h_scales)
+            nc.vector.quantize_mx(
+                out=codes[:, i, passes, :].rearrange("p g n -> p (g n)").bitcast(FP8X4),
+                scales=scales[:, i, passes, :].rearrange("p g n -> p (g n)"),
+                in_=grouped_tiles[n][:].rearrange("p g n j -> p (g n j)"),
+            )
+
+        def multiply(n):
+            kind, i, kc = stream[n]
+            for ct, b in units_of(kind, i):
+                if kc == 0:
+                    logits[(ct, b)] = psum.tile([P, BANK], F32, tag="bank", name="unit_logits")
+                for g in range(kc * CHUNK, (kc + 1) * CHUNK):
+                    nc.tensor.matmul_mx(
+                        out=logits[(ct, b)][:, 0:T],
+                        lhsT=w_codes[:, ct, g, :].bitcast(FP8X4),
+                        lhsT_scale=w_scales[:, ct, g, :],
+                        rhs=h_codes[:, b, g, :].bitcast(FP8X4),
+                        rhs_scale=h_scales[:, b, g, :],
+                        start=(g == 0),
+                        stop=(g == PASSES - 1),
+                    )
+
+        def exponentials(n):
+            kind, i, kc = stream[n]
+            if kc != CHUNKS - 1:
+                return
+            for ct, b in units_of(kind, i):
+                negated = frames.tile([P, T], F32, tag="negated")
+                nc.vector.scalar_tensor_tensor(
+                    out=negated[:],
+                    in0=logits[(ct, b)][:, 0:T],
+                    scalar=-1.0,
+                    in1=masked_add[:, b, :],
+                    op0=ALU.mult,
+                    op1=ALU.add,
+                )
+                nc.vector.tensor_reduce(
+                    out=neg_max[:, b, ct : ct + 1], in_=negated[:], axis=AXIS.X, op=ALU.min
+                )
+                e = frames.tile([P, T], F32, tag="e")
+                nc.scalar.activation(
+                    out=e[:],
+                    in_=negated[:],
+                    func=ACT.Exp,
+                    scale=-1.0,
+                    bias=neg_max[:, b, ct : ct + 1],
+                    accum_out=sum_e[:, b, ct : ct + 1],
+                )
+                e_tiles[(ct, b)] = e
+
+        def weighted_sums(n):
+            kind, i, kc = stream[n]
+            if kc != CHUNKS - 1:
+                return
+            ex_tiles = {}
+            for ct, b in units_of(kind, i):
+                ex = frames.tile([P, T], F32, tag="ex")
+                nc.vector.scalar_tensor_tensor(
+                    out=ex[:],
+                    in0=e_tiles[(ct, b)][:],
+                    scalar=1.0,
+                    in1=x_sb[:, b, ct, :],
+                    op0=ALU.mult,
+                    op1=ALU.mult,
+                    accum_out=sum_ex[:, b, ct : ct + 1],
+                )
+                ex_tiles[(ct, b)] = ex
+            for ct, b in units_of(kind, i):
+                exx = frames.tile([P, T], F32, tag="exx")
+                nc.vector.scalar_tensor_tensor(
+                    out=exx[:],
+                    in0=ex_tiles[(ct, b)][:],
+                    scalar=1.0,
+                    in1=x_sb[:, b, ct, :],
+                    op0=ALU.mult,
+                    op1=ALU.mult,
+                    accum_out=sum_exx[:, b, ct : ct + 1],
+                )
+
+        for n in range(AHEAD):
+            load(n)
+        for n in range(n_chunks + 3):
+            if n + AHEAD < n_chunks:
+                load(n + AHEAD)
+            if n < n_chunks:
+                group(n)
+            if 1 <= n <= n_chunks:
+                quantise(n - 1)
+                multiply(n - 1)
+            if 2 <= n <= n_chunks + 1:
+                exponentials(n - 2)
+            if 3 <= n:
+                weighted_sums(n - 3)
+
+        gain_rows = keep.tile([B * ROWS, P], BF16)
+        bias_rows = keep.tile([B * ROWS, P], BF16)
+        for b in range(B):
+            rows = slice(b * ROWS, (b + 1) * ROWS)
+            nc.sync.dma_start(out=gain_rows[rows, :], in_=g2.rearrange("(r p) -> r p", p=P))
+            nc.sync.dma_start(out=bias_rows[rows, :], in_=be2.rearrange("(r p) -> r p", p=P))
+
+        nc.scalar.activation(
+            out=table_warmer[:], in_=sum_e[:, B - 1, C_TILES - 1 : C_TILES], func=ACT.Sqrt
+        )
+        v = small.tile([P, B, 2, C_TILES], F32)
+        inv_sum_e = small.tile([P, B, C_TILES], F32)
+        nc.vector.reciprocal(out=inv_sum_e[:], in_=sum_e[:])
+        nc.vector.tensor_tensor(out=v[:, :, 0, :], in0=sum_ex[:], in1=inv_sum_e[:], op=ALU.mult)
+        second_moment = small.tile([P, B, C_TILES], F32)
+        nc.vector.tensor_tensor(out=second_moment[:], in0=sum_exx[:], in1=inv_sum_e[:], op=ALU.mult)
+        mean_squared = small.tile([P, B, C_TILES], F32)
+        nc.vector.tensor_tensor(out=mean_squared[:], in0=v[:, :, 0, :], in1=v[:, :, 0, :], op=ALU.mult)
+        variance = small.tile([P, B, C_TILES], F32)
+        nc.vector.tensor_tensor(out=variance[:], in0=second_moment[:], in1=mean_squared[:], op=ALU.subtract)
+        floored = small.tile([P, B, C_TILES], F32)
+        nc.vector.tensor_scalar_max(out=floored[:], in0=variance[:], scalar1=EPS_STD)
+        deviation = small.tile([P, B, C_TILES], F32)
+        nc.scalar.sqrt(out=deviation[:], in_=floored[:])
+        nc.vector.tensor_copy(out=v[:, :, 1, :], in_=deviation[:])
+
+        v_rows = v[:].rearrange("p b s ct -> p b (s ct)")
+        partial = small.tile([P, 2, B], F32)
+        nc.vector.tensor_reduce(out=partial[:, 0, :], in_=v_rows, axis=AXIS.X, op=ALU.add)
+        v_squared = small.tile([P, B, ROWS], F32)
+        nc.vector.tensor_tensor(out=v_squared[:], in0=v_rows, in1=v_rows, op=ALU.mult)
+        nc.vector.tensor_reduce(out=partial[:, 1, :], in_=v_squared[:], axis=AXIS.X, op=ALU.add)
+        averages_bank = psum.tile([P, BANK], F32, tag="bank")
+        nc.tensor.matmul(
+            out=averages_bank[:, 0 : 2 * B],
+            lhsT=averager[:],
+            rhs=partial[:].rearrange("p m b -> p (m b)"),
+            start=True,
+            stop=True,
+        )
+        averages = small.tile([P, 2, B], F32)
+        nc.vector.tensor_copy(out=averages[:].rearrange("p m b -> p (m b)"), in_=averages_bank[:, 0 : 2 * B])
+        mu = averages[:, 0, :]
+        minus_mu_squared = small.tile([P, B], F32)
+        nc.vector.scalar_tensor_tensor(
+            out=minus_mu_squared[:], in0=mu, scalar=-1.0, in1=mu, op0=ALU.mult, op1=ALU.mult
+        )
+        var_eps = small.tile([P, B], F32)
+        nc.vector.scalar_tensor_tensor(
+            out=var_eps[:],
+            in0=minus_mu_squared[:],
+            scalar=EPS_LN,
+            in1=averages[:, 1, :],
+            op0=ALU.add,
+            op1=ALU.add,
+        )
+        ln_deviation = small.tile([P, B], F32)
+        nc.scalar.sqrt(out=ln_deviation[:], in_=var_eps[:])
+        centred = small.tile([P, B, ROWS], F32)
+        nc.vector.tensor_tensor(
+            out=centred[:], in0=v_rows, in1=mu.unsqueeze(2).to_broadcast([P, B, ROWS]), op=ALU.subtract
+        )
+        inv_deviation = small.tile([P, B], F32)
+        nc.vector.reciprocal(out=inv_deviation[:], in_=ln_deviation[:])
+        nc.vector.tensor_tensor(
+            out=normed[:, 0 : B * ROWS].rearrange("p (b r) -> p b r", b=B),
+            in0=centred[:],
+            in1=inv_deviation[:].unsqueeze(2).to_broadcast([P, B, ROWS]),
+            op=ALU.mult,
+        )
+
+        normed_rows = psum.tile([P, BANK], F32, tag="bank")
+        nc.tensor.transpose(normed_rows[:, 0:P], normed[:], identity[:])
+        scaled = small.tile([B * ROWS, P], F32)
+        nc.vector.tensor_tensor(
+            out=scaled[:], in0=normed_rows[0 : B * ROWS, 0:P], in1=gain_rows[:], op=ALU.mult
+        )
+        result = small.tile([B * ROWS, P], F32)
+        nc.vector.tensor_tensor(out=result[:], in0=scaled[:], in1=bias_rows[:], op=ALU.add)
+        nc.sync.dma_start(out=out.rearrange("b (r p) o -> (b r) (p o)", p=P), in_=result[:])

@@ -44,7 +44,6 @@ def tile_attentivestatspool_pb_k_kernel(tc, h, x, mask, w2, b2, g2, be2, out):
         frames = ctx.enter_context(tc.tile_pool(name="frames", bufs=C_TILES))
         psum = ctx.enter_context(tc.psum_pool(name="psum", bufs=8))
         small = ctx.enter_context(tc.tile_pool(name="small", bufs=1))
-        ctx.enter_context(tc.manual_schedule())
 
         w_codes = keep.tile([P, C_TILES, PASSES, P], U32, align_bytes=64)
         w_scales = keep.tile([P, C_TILES, PASSES, P], U8, align_bytes=64)

@@ -27,9 +27,9 @@ K_CHUNK = CHUNK * K_PASS
 BANK = 512
 ROWS = 2 * C_TILES
 
-VECTOR_FRAMES = 112
+VECTOR_FRAMES = (144, 112, 96, 80)
 RUN = 4
-AHEAD = 3
+RAW_BUFS = 4
 MASKED = 1.0e30
 
 FLOPS = 2 * B * C * H * T
@@ -39,9 +39,9 @@ def tile_attentivestatspool_pb_k_kernel(tc, h, x, mask, w2, b2, g2, be2, out):
     nc = tc.nc
     with ExitStack() as ctx:
         keep = ctx.enter_context(tc.tile_pool(name="keep", bufs=1))
-        raw = ctx.enter_context(tc.tile_pool(name="raw", bufs=AHEAD))
+        raw = ctx.enter_context(tc.tile_pool(name="raw", bufs=RAW_BUFS))
         grouped = ctx.enter_context(tc.tile_pool(name="grouped", bufs=3))
-        frames = ctx.enter_context(tc.tile_pool(name="frames", bufs=C_TILES))
+        frames = ctx.enter_context(tc.tile_pool(name="frames", bufs=3))
         psum = ctx.enter_context(tc.psum_pool(name="psum", bufs=8))
         small = ctx.enter_context(tc.tile_pool(name="small", bufs=1))
 
@@ -59,7 +59,7 @@ def tile_attentivestatspool_pb_k_kernel(tc, h, x, mask, w2, b2, g2, be2, out):
         identity = keep.tile([P, P], F32)
         make_identity(nc, identity[:])
         mask_rows = keep.tile([P, B * T], BF16)
-        nc.vector.memset(mask_rows[:], 0.0)
+        nc.gpsimd.memset(mask_rows[:], 0.0)
         nc.scalar.dma_start(out=mask_rows[0:1, :], in_=mask.rearrange("b o t -> o (b t)"))
         ones = keep.tile([P, P], BF16)
         nc.vector.memset(ones[:], 1.0)
@@ -74,20 +74,22 @@ def tile_attentivestatspool_pb_k_kernel(tc, h, x, mask, w2, b2, g2, be2, out):
         nc.scalar.activation(out=table_warmer[:], in_=one_column[:], func=ACT.Exp)
 
         masked_add_flat = masked_add[:].rearrange("p b t -> p (b t)")
-        for half in range(B * T // BANK):
-            cols = slice(half * BANK, (half + 1) * BANK)
-            mask_everywhere = psum.tile([P, BANK], F32, tag="bank")
-            nc.tensor.matmul(
-                out=mask_everywhere[:], lhsT=ones[:], rhs=mask_rows[:, cols], start=True, stop=True
-            )
-            nc.vector.tensor_scalar(
-                out=masked_add_flat[:, cols],
-                in0=mask_everywhere[:],
-                scalar1=0.0,
-                scalar2=MASKED,
-                op0=ALU.is_equal,
-                op1=ALU.mult,
-            )
+
+        def spread_mask():
+            for half in range(B * T // BANK):
+                cols = slice(half * BANK, (half + 1) * BANK)
+                mask_everywhere = psum.tile([P, BANK], F32, tag="bank")
+                nc.tensor.matmul(
+                    out=mask_everywhere[:], lhsT=ones[:], rhs=mask_rows[:, cols], start=True, stop=True
+                )
+                nc.vector.tensor_scalar(
+                    out=masked_add_flat[:, cols],
+                    in0=mask_everywhere[:],
+                    scalar1=0.0,
+                    scalar2=MASKED,
+                    op0=ALU.is_equal,
+                    op1=ALU.mult,
+                )
 
         stream = []
         for i in range(B):
@@ -96,9 +98,14 @@ def tile_attentivestatspool_pb_k_kernel(tc, h, x, mask, w2, b2, g2, be2, out):
         n_chunks = len(stream)
 
         raw_tiles = {}
+        transposed_banks = {}
         grouped_tiles = {}
         logits = {}
+        negated_tiles = {}
         e_tiles = {}
+        finished = []
+        negated_units = []
+        weighted_units = []
 
         def units_of(kind, i):
             if kind == "w":
@@ -124,19 +131,27 @@ def tile_attentivestatspool_pb_k_kernel(tc, h, x, mask, w2, b2, g2, be2, out):
                 )
                 raw_tiles[n] = h_raw
 
+        def transpose(n):
+            kind, i, kc = stream[n]
+            if kind == "h":
+                return
+            words = raw_tiles[n][:].bitcast(F32).rearrange("c (g q u) -> c g u q", g=CHUNK, u=2)
+            transposed_banks[n] = []
+            for pair in range(CHUNK // 2):
+                transposed = psum.tile([P, 2, 2, P], F32, tag="bank")
+                for g in range(2):
+                    for u in range(2):
+                        nc.tensor.transpose(
+                            transposed[:, g, u, :], words[:, 2 * pair + g, u, :], identity[:]
+                        )
+                transposed_banks[n].append(transposed)
+
         def group(n):
             kind, i, kc = stream[n]
             if kind == "w":
                 w_grouped = grouped.tile([P, CHUNK, P, PACK], BF16, tag="w_grouped", align_bytes=64)
-                words = raw_tiles[n][:].bitcast(F32).rearrange("c (g q u) -> c g u q", g=CHUNK, u=2)
                 grouped_words = w_grouped[:].bitcast(F32)
-                for pair in range(CHUNK // 2):
-                    transposed = psum.tile([P, 2, 2, P], F32, tag="bank")
-                    for g in range(2):
-                        for u in range(2):
-                            nc.tensor.transpose(
-                                transposed[:, g, u, :], words[:, 2 * pair + g, u, :], identity[:]
-                            )
+                for pair, transposed in enumerate(transposed_banks[n]):
                     nc.scalar.copy(
                         out=grouped_words[:, 2 * pair : 2 * pair + 2, :, :],
                         in_=transposed[:].rearrange("q g u c -> q g c u"),
@@ -146,7 +161,7 @@ def tile_attentivestatspool_pb_k_kernel(tc, h, x, mask, w2, b2, g2, be2, out):
                 h_grouped = grouped.tile([P, CHUNK, T, PACK], BF16, tag="h_grouped", align_bytes=64)
                 src = raw_tiles[n][:].rearrange("p g j (c r) -> p g c j r", r=RUN)
                 dst = h_grouped[:].rearrange("p g (c r) j -> p g c j r", r=RUN)
-                split = VECTOR_FRAMES // RUN
+                split = VECTOR_FRAMES[i] // RUN
                 nc.vector.tensor_copy(out=dst[:, :, 0:split], in_=src[:, :, 0:split])
                 for g in range(CHUNK):
                     nc.scalar.copy(out=dst[:, g, split:], in_=src[:, g, split:])
@@ -177,41 +192,41 @@ def tile_attentivestatspool_pb_k_kernel(tc, h, x, mask, w2, b2, g2, be2, out):
                         start=(g == 0),
                         stop=(g == PASSES - 1),
                     )
+                if kc == CHUNKS - 1:
+                    finished.append((ct, b))
 
-        def exponentials(n):
-            kind, i, kc = stream[n]
-            if kc != CHUNKS - 1:
-                return
-            for ct, b in units_of(kind, i):
-                negated = frames.tile([P, T], F32, tag="negated")
-                nc.vector.scalar_tensor_tensor(
-                    out=negated[:],
-                    in0=logits[(ct, b)][:, 0:T],
-                    scalar=-1.0,
-                    in1=masked_add[:, b, :],
-                    op0=ALU.mult,
-                    op1=ALU.add,
-                )
-                nc.vector.tensor_reduce(
-                    out=neg_max[:, b, ct : ct + 1], in_=negated[:], axis=AXIS.X, op=ALU.min
-                )
-                e = frames.tile([P, T], F32, tag="e")
-                nc.scalar.activation(
-                    out=e[:],
-                    in_=negated[:],
-                    func=ACT.Exp,
-                    scale=-1.0,
-                    bias=neg_max[:, b, ct : ct + 1],
-                    accum_out=sum_e[:, b, ct : ct + 1],
-                )
-                e_tiles[(ct, b)] = e
+        def find_maximum(ct, b):
+            negated = frames.tile([P, T], F32, tag="negated")
+            nc.vector.scalar_tensor_tensor(
+                out=negated[:],
+                in0=logits[(ct, b)][:, 0:T],
+                scalar=-1.0,
+                in1=masked_add[:, b, :],
+                op0=ALU.mult,
+                op1=ALU.add,
+            )
+            nc.vector.tensor_reduce(
+                out=neg_max[:, b, ct : ct + 1], in_=negated[:], axis=AXIS.X, op=ALU.min
+            )
+            negated_tiles[(ct, b)] = negated
+            negated_units.append((ct, b))
 
-        def weighted_sums(n):
-            kind, i, kc = stream[n]
-            if kc != CHUNKS - 1:
-                return
+        def exponentials(ct, b):
+            e = frames.tile([P, T], F32, tag="e")
+            nc.scalar.activation(
+                out=e[:],
+                in_=negated_tiles[(ct, b)][:],
+                func=ACT.Exp,
+                scale=-1.0,
+                bias=neg_max[:, b, ct : ct + 1],
+                accum_out=sum_e[:, b, ct : ct + 1],
+            )
+            e_tiles[(ct, b)] = e
+            weighted_units.append((ct, b))
+
+        def weighted_sums(units):
             ex_tiles = {}
-            for ct, b in units_of(kind, i):
+            for ct, b in units:
                 ex = frames.tile([P, T], F32, tag="ex")
                 nc.vector.scalar_tensor_tensor(
                     out=ex[:],
@@ -223,7 +238,7 @@ def tile_attentivestatspool_pb_k_kernel(tc, h, x, mask, w2, b2, g2, be2, out):
                     accum_out=sum_ex[:, b, ct : ct + 1],
                 )
                 ex_tiles[(ct, b)] = ex
-            for ct, b in units_of(kind, i):
+            for ct, b in units:
                 exx = frames.tile([P, T], F32, tag="exx")
                 nc.vector.scalar_tensor_tensor(
                     out=exx[:],
@@ -235,20 +250,40 @@ def tile_attentivestatspool_pb_k_kernel(tc, h, x, mask, w2, b2, g2, be2, out):
                     accum_out=sum_exx[:, b, ct : ct + 1],
                 )
 
-        for n in range(AHEAD):
-            load(n)
-        for n in range(n_chunks + 3):
-            if n + AHEAD < n_chunks:
-                load(n + AHEAD)
-            if n < n_chunks:
+        def take(units):
+            taken = units[:]
+            units.clear()
+            return taken
+
+        n_loaded = 0
+        n_wanted = {"w": RAW_BUFS, "h": RAW_BUFS}
+        for n in range(-1, n_chunks + 2):
+            while n_loaded < n_chunks and n_wanted[stream[n_loaded][0]] > 0:
+                n_wanted[stream[n_loaded][0]] -= 1
+                load(n_loaded)
+                n_loaded += 1
+            if n + 1 < n_chunks:
+                transpose(n + 1)
+            if n == CHUNKS:
+                spread_mask()
+            if 0 <= n < n_chunks:
                 group(n)
+                n_wanted[stream[n][0]] += 1
+            weighted_sums(take(weighted_units))
+            for ct, b in take(negated_units):
+                exponentials(ct, b)
             if 1 <= n <= n_chunks:
                 quantise(n - 1)
-                multiply(n - 1)
-            if 2 <= n <= n_chunks + 1:
-                exponentials(n - 2)
-            if 3 <= n:
-                weighted_sums(n - 3)
+            if 2 <= n:
+                multiply(n - 2)
+            if finished and n < n_chunks:
+                find_maximum(*finished.pop(0))
+        for ct, b in take(negated_units):
+            exponentials(ct, b)
+        for ct, b in take(finished):
+            find_maximum(ct, b)
+            exponentials(ct, b)
+        weighted_sums(take(weighted_units))
 
         gain_rows = keep.tile([B * ROWS, P], BF16)
         bias_rows = keep.tile([B * ROWS, P], BF16)

@@ -59,21 +59,29 @@ def tile_attentivestatspool_pb_k_kernel(tc, h, x, mask, w2, b2, g2, be2, out):
         identity = keep.tile([P, P], F32)
         make_identity(nc, identity[:])
         mask_rows = keep.tile([P, B * T], BF16)
-        nc.gpsimd.memset(mask_rows[:], 0.0)
+        nc.vector.memset(mask_rows[:], 0.0)
         nc.scalar.dma_start(out=mask_rows[0:1, :], in_=mask.rearrange("b o t -> o (b t)"))
         ones = keep.tile([P, P], BF16)
         nc.vector.memset(ones[:], 1.0)
-        averager = keep.tile([P, P], F32)
-        nc.vector.memset(averager[:], 1.0 / (2 * C))
         one_column = keep.tile([P, 1], F32)
         nc.vector.memset(one_column[:], 1.0)
-        normed = keep.tile([P, P], F32)
-        nc.vector.memset(normed[:], 0.0)
+        averager = keep.tile([P, 1], F32)
+        nc.gpsimd.memset(averager[:], 1.0 / (2 * C))
+        eps_column = keep.tile([P, 1], F32)
+        nc.gpsimd.memset(eps_column[:], EPS_LN)
+        v_wide = keep.tile([P, P], F32)
+        nc.gpsimd.memset(v_wide[:], 0.0)
+        sums_wide = keep.tile([P, P], F32)
+        nc.gpsimd.memset(sums_wide[:], 0.0)
+        squares_wide = keep.tile([P, P], F32)
+        nc.gpsimd.memset(squares_wide[:], 0.0)
 
         table_warmer = keep.tile([P, 1], F32)
         nc.scalar.activation(out=table_warmer[:], in_=one_column[:], func=ACT.Exp)
 
         masked_add_flat = masked_add[:].rearrange("p b t -> p (b t)")
+
+        mask_banks = []
 
         def spread_mask():
             for half in range(B * T // BANK):
@@ -82,6 +90,11 @@ def tile_attentivestatspool_pb_k_kernel(tc, h, x, mask, w2, b2, g2, be2, out):
                 nc.tensor.matmul(
                     out=mask_everywhere[:], lhsT=ones[:], rhs=mask_rows[:, cols], start=True, stop=True
                 )
+                mask_banks.append(mask_everywhere)
+
+        def use_mask():
+            for half, mask_everywhere in enumerate(mask_banks):
+                cols = slice(half * BANK, (half + 1) * BANK)
                 nc.vector.tensor_scalar(
                     out=masked_add_flat[:, cols],
                     in0=mask_everywhere[:],
@@ -196,7 +209,7 @@ def tile_attentivestatspool_pb_k_kernel(tc, h, x, mask, w2, b2, g2, be2, out):
                     finished.append((ct, b))
 
         def find_maximum(ct, b):
-            negated = frames.tile([P, T], F32, tag="negated")
+            negated = frames.tile([P, T], F32, tag="negated", bufs=3)
             nc.vector.scalar_tensor_tensor(
                 out=negated[:],
                 in0=logits[(ct, b)][:, 0:T],
@@ -212,7 +225,7 @@ def tile_attentivestatspool_pb_k_kernel(tc, h, x, mask, w2, b2, g2, be2, out):
             negated_units.append((ct, b))
 
         def exponentials(ct, b):
-            e = frames.tile([P, T], F32, tag="e")
+            e = frames.tile([P, T], F32, tag="e", bufs=4)
             nc.scalar.activation(
                 out=e[:],
                 in_=negated_tiles[(ct, b)][:],
@@ -224,10 +237,10 @@ def tile_attentivestatspool_pb_k_kernel(tc, h, x, mask, w2, b2, g2, be2, out):
             e_tiles[(ct, b)] = e
             weighted_units.append((ct, b))
 
-        def weighted_sums(units):
+        def first_sums(units):
             ex_tiles = {}
             for ct, b in units:
-                ex = frames.tile([P, T], F32, tag="ex")
+                ex = frames.tile([P, T], F32, tag="ex", bufs=4)
                 nc.vector.scalar_tensor_tensor(
                     out=ex[:],
                     in0=e_tiles[(ct, b)][:],
@@ -238,8 +251,11 @@ def tile_attentivestatspool_pb_k_kernel(tc, h, x, mask, w2, b2, g2, be2, out):
                     accum_out=sum_ex[:, b, ct : ct + 1],
                 )
                 ex_tiles[(ct, b)] = ex
+            return ex_tiles
+
+        def second_sums(units, ex_tiles):
             for ct, b in units:
-                exx = frames.tile([P, T], F32, tag="exx")
+                exx = frames.tile([P, T], F32, tag="exx", bufs=1)
                 nc.vector.scalar_tensor_tensor(
                     out=exx[:],
                     in0=ex_tiles[(ct, b)][:],
@@ -250,118 +266,137 @@ def tile_attentivestatspool_pb_k_kernel(tc, h, x, mask, w2, b2, g2, be2, out):
                     accum_out=sum_exx[:, b, ct : ct + 1],
                 )
 
+        def weighted_sums(units):
+            second_sums(units, first_sums(units))
+
         def take(units):
             taken = units[:]
             units.clear()
             return taken
 
-        n_loaded = 0
-        n_wanted = {"w": RAW_BUFS, "h": RAW_BUFS}
-        for n in range(-1, n_chunks + 2):
-            while n_loaded < n_chunks and n_wanted[stream[n_loaded][0]] > 0:
-                n_wanted[stream[n_loaded][0]] -= 1
-                load(n_loaded)
-                n_loaded += 1
-            if n + 1 < n_chunks:
-                transpose(n + 1)
-            if n == CHUNKS:
-                spread_mask()
-            if 0 <= n < n_chunks:
-                group(n)
-                n_wanted[stream[n][0]] += 1
-            weighted_sums(take(weighted_units))
-            for ct, b in take(negated_units):
-                exponentials(ct, b)
-            if 1 <= n <= n_chunks:
-                quantise(n - 1)
-            if 2 <= n:
-                multiply(n - 2)
-            if finished and n < n_chunks:
-                find_maximum(*finished.pop(0))
-        for ct, b in take(negated_units):
-            exponentials(ct, b)
-        for ct, b in take(finished):
-            find_maximum(ct, b)
-            exponentials(ct, b)
-        weighted_sums(take(weighted_units))
-
         gain_rows = keep.tile([B * ROWS, P], BF16)
         bias_rows = keep.tile([B * ROWS, P], BF16)
-        for b in range(B):
-            rows = slice(b * ROWS, (b + 1) * ROWS)
-            nc.sync.dma_start(out=gain_rows[rows, :], in_=g2.rearrange("(r p) -> r p", p=P))
-            nc.sync.dma_start(out=bias_rows[rows, :], in_=be2.rearrange("(r p) -> r p", p=P))
 
-        nc.scalar.activation(
-            out=table_warmer[:], in_=sum_e[:, B - 1, C_TILES - 1 : C_TILES], func=ACT.Sqrt
-        )
-        v = small.tile([P, B, 2, C_TILES], F32)
-        inv_sum_e = small.tile([P, B, C_TILES], F32)
-        nc.vector.reciprocal(out=inv_sum_e[:], in_=sum_e[:])
-        nc.vector.tensor_tensor(out=v[:, :, 0, :], in0=sum_ex[:], in1=inv_sum_e[:], op=ALU.mult)
-        second_moment = small.tile([P, B, C_TILES], F32)
-        nc.vector.tensor_tensor(out=second_moment[:], in0=sum_exx[:], in1=inv_sum_e[:], op=ALU.mult)
-        mean_squared = small.tile([P, B, C_TILES], F32)
-        nc.vector.tensor_tensor(out=mean_squared[:], in0=v[:, :, 0, :], in1=v[:, :, 0, :], op=ALU.mult)
-        variance = small.tile([P, B, C_TILES], F32)
-        nc.vector.tensor_tensor(out=variance[:], in0=second_moment[:], in1=mean_squared[:], op=ALU.subtract)
-        floored = small.tile([P, B, C_TILES], F32)
-        nc.vector.tensor_scalar_max(out=floored[:], in0=variance[:], scalar1=EPS_STD)
-        deviation = small.tile([P, B, C_TILES], F32)
-        nc.scalar.sqrt(out=deviation[:], in_=floored[:])
-        nc.vector.tensor_copy(out=v[:, :, 1, :], in_=deviation[:])
+        def load_gain_and_bias():
+            for b in range(B):
+                rows = slice(b * ROWS, (b + 1) * ROWS)
+                nc.sync.dma_start(out=gain_rows[rows, :], in_=g2.rearrange("(r p) -> r p", p=P))
+                nc.sync.dma_start(out=bias_rows[rows, :], in_=be2.rearrange("(r p) -> r p", p=P))
 
-        v_rows = v[:].rearrange("p b s ct -> p b (s ct)")
-        partial = small.tile([P, 2, B], F32)
-        nc.vector.tensor_reduce(out=partial[:, 0, :], in_=v_rows, axis=AXIS.X, op=ALU.add)
-        v_squared = small.tile([P, B, ROWS], F32)
-        nc.vector.tensor_tensor(out=v_squared[:], in0=v_rows, in1=v_rows, op=ALU.mult)
-        nc.vector.tensor_reduce(out=partial[:, 1, :], in_=v_squared[:], axis=AXIS.X, op=ALU.add)
-        averages_bank = psum.tile([P, BANK], F32, tag="bank")
-        nc.tensor.matmul(
-            out=averages_bank[:, 0 : 2 * B],
-            lhsT=averager[:],
-            rhs=partial[:].rearrange("p m b -> p (m b)"),
-            start=True,
-            stop=True,
-        )
-        averages = small.tile([P, 2, B], F32)
-        nc.vector.tensor_copy(out=averages[:].rearrange("p m b -> p (m b)"), in_=averages_bank[:, 0 : 2 * B])
-        mu = averages[:, 0, :]
-        minus_mu_squared = small.tile([P, B], F32)
-        nc.vector.scalar_tensor_tensor(
-            out=minus_mu_squared[:], in0=mu, scalar=-1.0, in1=mu, op0=ALU.mult, op1=ALU.mult
-        )
-        var_eps = small.tile([P, B], F32)
-        nc.vector.scalar_tensor_tensor(
-            out=var_eps[:],
-            in0=minus_mu_squared[:],
-            scalar=EPS_LN,
-            in1=averages[:, 1, :],
-            op0=ALU.add,
-            op1=ALU.add,
-        )
-        ln_deviation = small.tile([P, B], F32)
-        nc.scalar.sqrt(out=ln_deviation[:], in_=var_eps[:])
-        centred = small.tile([P, B, ROWS], F32)
-        nc.vector.tensor_tensor(
-            out=centred[:], in0=v_rows, in1=mu.unsqueeze(2).to_broadcast([P, B, ROWS]), op=ALU.subtract
-        )
-        inv_deviation = small.tile([P, B], F32)
-        nc.vector.reciprocal(out=inv_deviation[:], in_=ln_deviation[:])
-        nc.vector.tensor_tensor(
-            out=normed[:, 0 : B * ROWS].rearrange("p (b r) -> p b r", b=B),
-            in0=centred[:],
-            in1=inv_deviation[:].unsqueeze(2).to_broadcast([P, B, ROWS]),
-            op=ALU.mult,
-        )
+        n_loaded = 0
+        n_wanted = {"w": RAW_BUFS, "h": RAW_BUFS}
+        with tc.manual_schedule():
+            for n in range(-1, n_chunks + 2):
+                while n_loaded < n_chunks and n_wanted[stream[n_loaded][0]] > 0:
+                    n_wanted[stream[n_loaded][0]] -= 1
+                    load(n_loaded)
+                    n_loaded += 1
+                if n + 1 < n_chunks:
+                    transpose(n + 1)
+                if n == CHUNKS + 3:
+                    spread_mask()
+                if 0 <= n < n_chunks:
+                    group(n)
+                    n_wanted[stream[n][0]] += 1
+                to_weigh = take(weighted_units)
+                for ct, b in take(negated_units):
+                    exponentials(ct, b)
+                if finished and n < n_chunks:
+                    find_maximum(*finished.pop(0))
+                if 1 <= n <= n_chunks:
+                    quantise(n - 1)
+                weighted_sums(to_weigh)
+                if n == CHUNKS + 4:
+                    use_mask()
+                if 2 <= n:
+                    multiply(n - 2)
+            load_gain_and_bias()
+            to_weigh = take(weighted_units)
+            for ct, b in take(negated_units):
+                exponentials(ct, b)
+            weighted_sums(to_weigh)
+            while finished:
+                to_weigh = take(weighted_units)
+                for ct, b in finished[:C_TILES]:
+                    find_maximum(ct, b)
+                    exponentials(ct, b)
+                finished = finished[C_TILES:]
+                weighted_sums(to_weigh)
 
-        normed_rows = psum.tile([P, BANK], F32, tag="bank")
-        nc.tensor.transpose(normed_rows[:, 0:P], normed[:], identity[:])
-        scaled = small.tile([B * ROWS, P], F32)
-        nc.vector.tensor_tensor(
-            out=scaled[:], in0=normed_rows[0 : B * ROWS, 0:P], in1=gain_rows[:], op=ALU.mult
-        )
-        result = small.tile([B * ROWS, P], F32)
-        nc.vector.tensor_tensor(out=result[:], in0=scaled[:], in1=bias_rows[:], op=ALU.add)
-        nc.sync.dma_start(out=out.rearrange("b (r p) o -> (b r) (p o)", p=P), in_=result[:])
+            nc.scalar.activation(
+                out=table_warmer[:], in_=sum_e[:, B - 1, C_TILES - 1 : C_TILES], func=ACT.Sqrt
+            )
+            ex_tiles = first_sums(weighted_units)
+
+            v = v_wide[:, 0 : B * ROWS].rearrange("p (b s ct) -> p b s ct", b=B, s=2)
+            squares = small.tile([P, B, 2, C_TILES], F32)
+            inv_sum_e = small.tile([P, B, C_TILES], F32)
+            nc.vector.reciprocal(out=inv_sum_e[:], in_=sum_e[:])
+            nc.vector.tensor_tensor(out=v[:, :, 0, :], in0=sum_ex[:], in1=inv_sum_e[:], op=ALU.mult)
+            second_sums(weighted_units, ex_tiles)
+            nc.vector.tensor_tensor(out=squares[:, :, 0, :], in0=v[:, :, 0, :], in1=v[:, :, 0, :], op=ALU.mult)
+            second_moment = small.tile([P, B, C_TILES], F32)
+            nc.vector.tensor_tensor(out=second_moment[:], in0=sum_exx[:], in1=inv_sum_e[:], op=ALU.mult)
+            variance = small.tile([P, B, C_TILES], F32)
+            nc.vector.tensor_tensor(
+                out=variance[:], in0=second_moment[:], in1=squares[:, :, 0, :], op=ALU.subtract
+            )
+            nc.vector.tensor_scalar_max(out=squares[:, :, 1, :], in0=variance[:], scalar1=EPS_STD)
+            nc.scalar.sqrt(out=v[:, :, 1, :], in_=squares[:, :, 1, :])
+
+            def averages(wide, values, name):
+                eight = values.rearrange("p b s ct -> p b (s ct)").unsqueeze(2)
+                nc.vector.tensor_reduce(
+                    out=wide[:, 0 : B * ROWS].rearrange("p (b r) -> p b r", b=B),
+                    in_=eight.to_broadcast([P, B, ROWS, ROWS]),
+                    axis=AXIS.X,
+                    op=ALU.add,
+                )
+                average_bank = psum.tile([P, BANK], F32, tag="bank", name=name)
+                nc.tensor.matmul(
+                    out=average_bank[:, 0:1], lhsT=wide[:], rhs=averager[:], start=True, stop=True
+                )
+                return average_bank[0 : B * ROWS, 0:1]
+
+            mean_square = averages(squares_wide, squares[:], "mean_square_bank")
+            v_rows = psum.tile([P, BANK], F32, tag="bank")
+            nc.tensor.transpose(v_rows[:, 0:P], v_wide[:], identity[:])
+            mu = averages(sums_wide, v, "mu_bank")
+            negated_variance = small.tile([B * ROWS, 1], F32)
+            nc.vector.tensor_scalar(
+                out=negated_variance[:],
+                in0=mu,
+                scalar1=mu,
+                scalar2=mean_square,
+                op0=ALU.mult,
+                op1=ALU.subtract,
+            )
+            ln_deviation = small.tile([B * ROWS, 1], F32)
+            nc.scalar.activation(
+                out=ln_deviation[:],
+                in_=negated_variance[:],
+                func=ACT.Sqrt,
+                scale=-1.0,
+                bias=eps_column[0 : B * ROWS, :],
+            )
+            scaled = small.tile([B * ROWS, P], F32)
+            nc.vector.scalar_tensor_tensor(
+                out=scaled[:],
+                in0=v_rows[0 : B * ROWS, 0:P],
+                scalar=mu,
+                in1=gain_rows[:],
+                op0=ALU.subtract,
+                op1=ALU.mult,
+            )
+            inv_deviation = small.tile([B * ROWS, 1], F32)
+            nc.vector.reciprocal(out=inv_deviation[:], in_=ln_deviation[:])
+            result = small.tile([B * ROWS, P], F32)
+            nc.vector.scalar_tensor_tensor(
+                out=result[:],
+                in0=scaled[:],
+                scalar=inv_deviation[:],
+                in1=bias_rows[:],
+                op0=ALU.mult,
+                op1=ALU.add,
+            )
+            nc.sync.dma_start(out=out.rearrange("b (r p) o -> (b r) (p o)", p=P), in_=result[:])

@@ -27,7 +27,7 @@ K_CHUNK = CHUNK * K_PASS
 BANK = 512
 ROWS = 2 * C_TILES
 
-VECTOR_FRAMES = (144, 112, 96, 80)
+VECTOR_FRAMES = (176, 144, 128, 112)
 RUN = 4
 RAW_BUFS = 4
 MASKED = 1.0e30
@@ -283,33 +283,39 @@ def tile_attentivestatspool_pb_k_kernel(tc, h, x, mask, w2, b2, g2, be2, out):
                 nc.sync.dma_start(out=gain_rows[rows, :], in_=g2.rearrange("(r p) -> r p", p=P))
                 nc.sync.dma_start(out=bias_rows[rows, :], in_=be2.rearrange("(r p) -> r p", p=P))
 
-        n_loaded = 0
+        n_loaded = [0]
         n_wanted = {"w": RAW_BUFS, "h": RAW_BUFS}
+        def step(n):
+            while n_loaded[0] < n_chunks and n_wanted[stream[n_loaded[0]][0]] > 0:
+                n_wanted[stream[n_loaded[0]][0]] -= 1
+                load(n_loaded[0])
+                n_loaded[0] += 1
+            if n + 1 < n_chunks:
+                transpose(n + 1)
+            if n == CHUNKS + 3:
+                spread_mask()
+            if 0 <= n < n_chunks:
+                group(n)
+                n_wanted[stream[n][0]] += 1
+            to_weigh = take(weighted_units)
+            for ct, b in take(negated_units):
+                exponentials(ct, b)
+            if finished and n < n_chunks:
+                find_maximum(*finished.pop(0))
+            if 1 <= n <= n_chunks:
+                quantise(n - 1)
+            weighted_sums(to_weigh)
+            if n == CHUNKS + 4:
+                use_mask()
+            if 2 <= n:
+                multiply(n - 2)
+
         with tc.manual_schedule():
-            for n in range(-1, n_chunks + 2):
-                while n_loaded < n_chunks and n_wanted[stream[n_loaded][0]] > 0:
-                    n_wanted[stream[n_loaded][0]] -= 1
-                    load(n_loaded)
-                    n_loaded += 1
-                if n + 1 < n_chunks:
-                    transpose(n + 1)
-                if n == CHUNKS + 3:
-                    spread_mask()
-                if 0 <= n < n_chunks:
-                    group(n)
-                    n_wanted[stream[n][0]] += 1
-                to_weigh = take(weighted_units)
-                for ct, b in take(negated_units):
-                    exponentials(ct, b)
-                if finished and n < n_chunks:
-                    find_maximum(*finished.pop(0))
-                if 1 <= n <= n_chunks:
-                    quantise(n - 1)
-                weighted_sums(to_weigh)
-                if n == CHUNKS + 4:
-                    use_mask()
-                if 2 <= n:
-                    multiply(n - 2)
+            for n in range(-1, CHUNKS):
+                step(n)
+        for n in range(CHUNKS, n_chunks + 2):
+            step(n)
+        with tc.manual_schedule():
             load_gain_and_bias()
             to_weigh = take(weighted_units)
             for ct, b in take(negated_units):

@@ -21,13 +21,12 @@ PACK = 4
 K_PASS = P * PACK
 PASSES = H // K_PASS
 C_TILES = C // P
-CHUNK = 4
-CHUNKS = PASSES // CHUNK
-K_CHUNK = CHUNK * K_PASS
+FIRST_CHUNKS = (2, 2, 4, 4, 4)
+CHUNKS = (4, 4, 4, 4)
 BANK = 512
 ROWS = 2 * C_TILES
 
-VECTOR_FRAMES = (176, 144, 128, 112)
+VECTOR_FRAMES = (160, 128, 112, 96)
 RUN = 4
 RAW_BUFS = 4
 MASKED = 1.0e30
@@ -104,10 +103,16 @@ def tile_attentivestatspool_pb_k_kernel(tc, h, x, mask, w2, b2, g2, be2, out):
                     op1=ALU.mult,
                 )
 
-        stream = []
-        for i in range(B):
-            stream.extend([("w", i, kc) for kc in range(CHUNKS)])
-            stream.extend([("h", i, kc) for kc in range(CHUNKS)])
+        def chunks_of(kind, i, sizes):
+            return [(kind, i, sum(sizes[:c]), sizes[c]) for c in range(len(sizes))]
+
+        def in_turn(one, other):
+            return [chunk for pair in zip(one, other) for chunk in pair]
+
+        stream = in_turn(chunks_of("h", 0, FIRST_CHUNKS), chunks_of("w", 0, FIRST_CHUNKS))
+        stream += in_turn(chunks_of("w", 1, CHUNKS), chunks_of("h", 1, CHUNKS))
+        for i in range(2, B):
+            stream += chunks_of("w", i, CHUNKS) + chunks_of("h", i, CHUNKS)
         n_chunks = len(stream)
 
         raw_tiles = {}
@@ -120,37 +125,39 @@ def tile_attentivestatspool_pb_k_kernel(tc, h, x, mask, w2, b2, g2, be2, out):
         negated_units = []
         weighted_units = []
 
-        def units_of(kind, i):
+        quantised = set()
+
+        def units_of(kind, i, g):
             if kind == "w":
-                return [(i, b) for b in range(i)]
-            return [(ct, i) for ct in range(i + 1)]
+                return [(i, b) for b in range(B) if ("h", b, g) in quantised]
+            return [(ct, i) for ct in range(C_TILES) if ("w", ct, g) in quantised]
 
         def load(n):
-            kind, i, kc = stream[n]
-            k_rows = slice(kc * K_CHUNK, (kc + 1) * K_CHUNK)
+            kind, i, first, passes = stream[n]
+            k_rows = slice(first * K_PASS, (first + passes) * K_PASS)
             if kind == "w":
-                w_raw = raw.tile([P, K_CHUNK], BF16, tag="w_raw")
+                w_raw = raw.tile([P, passes * K_PASS], BF16, tag="w_raw")
                 nc.sync.dma_start(out=w_raw[:], in_=w2[i * P : (i + 1) * P, k_rows])
                 raw_tiles[n] = w_raw
             else:
-                if kc == 0:
-                    nc.sync.dma_start(
-                        out=x_sb[:, i, :, :], in_=x[i].rearrange("(ct p) t -> p ct t", p=P)
-                    )
-                h_raw = raw.tile([P, CHUNK, PACK, T], BF16, tag="h_raw")
+                h_raw = raw.tile([P, passes, PACK, T], BF16, tag="h_raw")
                 nc.sync.dma_start(
                     out=h_raw[:],
                     in_=h[i, k_rows, :].rearrange("(g p j) t -> p g j t", p=P, j=PACK),
                 )
                 raw_tiles[n] = h_raw
+                if first + passes == PASSES:
+                    nc.sync.dma_start(
+                        out=x_sb[:, i, :, :], in_=x[i].rearrange("(ct p) t -> p ct t", p=P)
+                    )
 
         def transpose(n):
-            kind, i, kc = stream[n]
+            kind, i, first, passes = stream[n]
             if kind == "h":
                 return
-            words = raw_tiles[n][:].bitcast(F32).rearrange("c (g q u) -> c g u q", g=CHUNK, u=2)
+            words = raw_tiles[n][:].bitcast(F32).rearrange("c (g q u) -> c g u q", g=passes, u=2)
             transposed_banks[n] = []
-            for pair in range(CHUNK // 2):
+            for pair in range(passes // 2):
                 transposed = psum.tile([P, 2, 2, P], F32, tag="bank")
                 for g in range(2):
                     for u in range(2):
@@ -160,9 +167,9 @@ def tile_attentivestatspool_pb_k_kernel(tc, h, x, mask, w2, b2, g2, be2, out):
                 transposed_banks[n].append(transposed)
 
         def group(n):
-            kind, i, kc = stream[n]
+            kind, i, first, passes = stream[n]
             if kind == "w":
-                w_grouped = grouped.tile([P, CHUNK, P, PACK], BF16, tag="w_grouped", align_bytes=64)
+                w_grouped = grouped.tile([P, passes, P, PACK], BF16, tag="w_grouped", align_bytes=64)
                 grouped_words = w_grouped[:].bitcast(F32)
                 for pair, transposed in enumerate(transposed_banks[n]):
                     nc.scalar.copy(
@@ -171,18 +178,18 @@ def tile_attentivestatspool_pb_k_kernel(tc, h, x, mask, w2, b2, g2, be2, out):
                     )
                 grouped_tiles[n] = w_grouped
             else:
-                h_grouped = grouped.tile([P, CHUNK, T, PACK], BF16, tag="h_grouped", align_bytes=64)
+                h_grouped = grouped.tile([P, passes, T, PACK], BF16, tag="h_grouped", align_bytes=64)
                 src = raw_tiles[n][:].rearrange("p g j (c r) -> p g c j r", r=RUN)
                 dst = h_grouped[:].rearrange("p g (c r) j -> p g c j r", r=RUN)
                 split = VECTOR_FRAMES[i] // RUN
                 nc.vector.tensor_copy(out=dst[:, :, 0:split], in_=src[:, :, 0:split])
-                for g in range(CHUNK):
+                for g in range(passes):
                     nc.scalar.copy(out=dst[:, g, split:], in_=src[:, g, split:])
                 grouped_tiles[n] = h_grouped
 
         def quantise(n):
-            kind, i, kc = stream[n]
-            passes = slice(kc * CHUNK, (kc + 1) * CHUNK)
+            kind, i, first, n_passes = stream[n]
+            passes = slice(first, first + n_passes)
             codes, scales = (w_codes, w_scales) if kind == "w" else (h_codes, h_scales)
             nc.vector.quantize_mx(
                 out=codes[:, i, passes, :].rearrange("p g n -> p (g n)").bitcast(FP8X4),
@@ -191,11 +198,13 @@ def tile_attentivestatspool_pb_k_kernel(tc, h, x, mask, w2, b2, g2, be2, out):
             )
 
         def multiply(n):
-            kind, i, kc = stream[n]
-            for ct, b in units_of(kind, i):
-                if kc == 0:
+            kind, i, first, passes = stream[n]
+            for g in range(first, first + passes):
+                quantised.add((kind, i, g))
+            for ct, b in units_of(kind, i, first):
+                if first == 0:
                     logits[(ct, b)] = psum.tile([P, BANK], F32, tag="bank", name="unit_logits")
-                for g in range(kc * CHUNK, (kc + 1) * CHUNK):
+                for g in range(first, first + passes):
                     nc.tensor.matmul_mx(
                         out=logits[(ct, b)][:, 0:T],
                         lhsT=w_codes[:, ct, g, :].bitcast(FP8X4),
@@ -205,11 +214,11 @@ def tile_attentivestatspool_pb_k_kernel(tc, h, x, mask, w2, b2, g2, be2, out):
                         start=(g == 0),
                         stop=(g == PASSES - 1),
                     )
-                if kc == CHUNKS - 1:
+                if first + passes == PASSES:
                     finished.append((ct, b))
 
-        def find_maximum(ct, b):
-            negated = frames.tile([P, T], F32, tag="negated", bufs=3)
+        def negate(ct, b):
+            negated = frames.tile([P, T], F32, tag="negated", bufs=4)
             nc.vector.scalar_tensor_tensor(
                 out=negated[:],
                 in0=logits[(ct, b)][:, 0:T],
@@ -218,10 +227,12 @@ def tile_attentivestatspool_pb_k_kernel(tc, h, x, mask, w2, b2, g2, be2, out):
                 op0=ALU.mult,
                 op1=ALU.add,
             )
-            nc.vector.tensor_reduce(
-                out=neg_max[:, b, ct : ct + 1], in_=negated[:], axis=AXIS.X, op=ALU.min
-            )
             negated_tiles[(ct, b)] = negated
+
+        def find_maximum(ct, b):
+            nc.vector.tensor_reduce(
+                out=neg_max[:, b, ct : ct + 1], in_=negated_tiles[(ct, b)][:], axis=AXIS.X, op=ALU.min
+            )
             negated_units.append((ct, b))
 
         def exponentials(ct, b):
@@ -292,42 +303,49 @@ def tile_attentivestatspool_pb_k_kernel(tc, h, x, mask, w2, b2, g2, be2, out):
                 n_loaded[0] += 1
             if n + 1 < n_chunks:
                 transpose(n + 1)
-            if n == CHUNKS + 3:
+            if n == 7:
                 spread_mask()
+            to_weigh = take(weighted_units)
+            to_exponentiate = take(negated_units)
+            to_negate = [finished.pop(0)] if finished else []
+            for ct, b in to_negate:
+                negate(ct, b)
+            ex_tiles = first_sums(to_weigh)
             if 0 <= n < n_chunks:
                 group(n)
                 n_wanted[stream[n][0]] += 1
-            to_weigh = take(weighted_units)
-            for ct, b in take(negated_units):
+            for ct, b in to_exponentiate:
                 exponentials(ct, b)
-            if finished and n < n_chunks:
-                find_maximum(*finished.pop(0))
+            for ct, b in to_negate:
+                find_maximum(ct, b)
+            second_sums(to_weigh, ex_tiles)
             if 1 <= n <= n_chunks:
                 quantise(n - 1)
-            weighted_sums(to_weigh)
-            if n == CHUNKS + 4:
+            if n == 8:
                 use_mask()
             if 2 <= n:
                 multiply(n - 2)
 
         with tc.manual_schedule():
-            for n in range(-1, CHUNKS):
+            for n in range(-1, n_chunks + 2):
                 step(n)
-        for n in range(CHUNKS, n_chunks + 2):
-            step(n)
+
         with tc.manual_schedule():
             load_gain_and_bias()
             to_weigh = take(weighted_units)
+            last = take(finished)
             for ct, b in take(negated_units):
                 exponentials(ct, b)
+            negate(*last[0])
             weighted_sums(to_weigh)
-            while finished:
-                to_weigh = take(weighted_units)
-                for ct, b in finished[:C_TILES]:
-                    find_maximum(ct, b)
-                    exponentials(ct, b)
-                finished = finished[C_TILES:]
-                weighted_sums(to_weigh)
+            to_weigh = take(weighted_units)
+            for i, unit in enumerate(last):
+                if i + 1 < len(last):
+                    negate(*last[i + 1])
+                elif to_weigh:
+                    weighted_sums(to_weigh)
+                find_maximum(*unit)
+                exponentials(*take(negated_units)[0])
 
             nc.scalar.activation(
                 out=table_warmer[:], in_=sum_e[:, B - 1, C_TILES - 1 : C_TILES], func=ACT.Sqrt

@@ -26,7 +26,7 @@ CHUNKS = (4, 4, 4, 4)
 BANK = 512
 ROWS = 2 * C_TILES
 
-VECTOR_FRAMES = (160, 128, 112, 96)
+VECTOR_FRAMES = (160, 144, 104, 88)
 RUN = 4
 RAW_BUFS = 4
 MASKED = 1.0e30
@@ -106,13 +106,17 @@ def tile_attentivestatspool_pb_k_kernel(tc, h, x, mask, w2, b2, g2, be2, out):
         def chunks_of(kind, i, sizes):
             return [(kind, i, sum(sizes[:c]), sizes[c]) for c in range(len(sizes))]
 
-        def in_turn(one, other):
-            return [chunk for pair in zip(one, other) for chunk in pair]
+        def in_turn(*operands):
+            return [chunk for together in zip(*operands) for chunk in together]
 
-        stream = in_turn(chunks_of("h", 0, FIRST_CHUNKS), chunks_of("w", 0, FIRST_CHUNKS))
-        stream += in_turn(chunks_of("w", 1, CHUNKS), chunks_of("h", 1, CHUNKS))
-        for i in range(2, B):
-            stream += chunks_of("w", i, CHUNKS) + chunks_of("h", i, CHUNKS)
+        stream = in_turn(
+            chunks_of("w", 0, FIRST_CHUNKS), chunks_of("h", 0, FIRST_CHUNKS), chunks_of("w", 1, FIRST_CHUNKS)
+        )
+        for i in range(1, B):
+            if i + 1 < C_TILES:
+                stream += in_turn(chunks_of("w", i + 1, CHUNKS), chunks_of("h", i, CHUNKS))
+            else:
+                stream += chunks_of("h", i, CHUNKS)
         n_chunks = len(stream)
 
         raw_tiles = {}
@@ -266,7 +270,7 @@ def tile_attentivestatspool_pb_k_kernel(tc, h, x, mask, w2, b2, g2, be2, out):
 
         def second_sums(units, ex_tiles):
             for ct, b in units:
-                exx = frames.tile([P, T], F32, tag="exx", bufs=1)
+                exx = frames.tile([P, T], F32, tag="exx", bufs=2)
                 nc.vector.scalar_tensor_tensor(
                     out=exx[:],
                     in0=ex_tiles[(ct, b)][:],
@@ -301,21 +305,23 @@ def tile_attentivestatspool_pb_k_kernel(tc, h, x, mask, w2, b2, g2, be2, out):
                 n_wanted[stream[n_loaded[0]][0]] -= 1
                 load(n_loaded[0])
                 n_loaded[0] += 1
+                if n_loaded[0] == n_chunks:
+                    load_gain_and_bias()
             if n + 1 < n_chunks:
                 transpose(n + 1)
             if n == 7:
                 spread_mask()
             to_weigh = take(weighted_units)
             to_exponentiate = take(negated_units)
-            to_negate = [finished.pop(0)] if finished else []
+            to_negate = [finished.pop(0) for c in range(min(len(finished), 2))]
             for ct, b in to_negate:
                 negate(ct, b)
             ex_tiles = first_sums(to_weigh)
+            for ct, b in to_exponentiate:
+                exponentials(ct, b)
             if 0 <= n < n_chunks:
                 group(n)
                 n_wanted[stream[n][0]] += 1
-            for ct, b in to_exponentiate:
-                exponentials(ct, b)
             for ct, b in to_negate:
                 find_maximum(ct, b)
             second_sums(to_weigh, ex_tiles)
@@ -329,9 +335,6 @@ def tile_attentivestatspool_pb_k_kernel(tc, h, x, mask, w2, b2, g2, be2, out):
         with tc.manual_schedule():
             for n in range(-1, n_chunks + 2):
                 step(n)
-
-        with tc.manual_schedule():
-            load_gain_and_bias()
             to_weigh = take(weighted_units)
             last = take(finished)
             for ct, b in take(negated_units):
@@ -350,17 +353,35 @@ def tile_attentivestatspool_pb_k_kernel(tc, h, x, mask, w2, b2, g2, be2, out):
             nc.scalar.activation(
                 out=table_warmer[:], in_=sum_e[:, B - 1, C_TILES - 1 : C_TILES], func=ACT.Sqrt
             )
-            ex_tiles = first_sums(weighted_units)
-
             v = v_wide[:, 0 : B * ROWS].rearrange("p (b s ct) -> p b s ct", b=B, s=2)
             squares = small.tile([P, B, 2, C_TILES], F32)
             inv_sum_e = small.tile([P, B, C_TILES], F32)
-            nc.vector.reciprocal(out=inv_sum_e[:], in_=sum_e[:])
-            nc.vector.tensor_tensor(out=v[:, :, 0, :], in0=sum_ex[:], in1=inv_sum_e[:], op=ALU.mult)
-            second_sums(weighted_units, ex_tiles)
-            nc.vector.tensor_tensor(out=squares[:, :, 0, :], in0=v[:, :, 0, :], in1=v[:, :, 0, :], op=ALU.mult)
             second_moment = small.tile([P, B, C_TILES], F32)
-            nc.vector.tensor_tensor(out=second_moment[:], in0=sum_exx[:], in1=inv_sum_e[:], op=ALU.mult)
+            ex_tiles = first_sums(weighted_units[:-1])
+            nc.vector.reciprocal(out=inv_sum_e[:], in_=sum_e[:])
+            ex_tiles.update(first_sums(weighted_units[-1:]))
+            nc.vector.tensor_tensor(
+                out=second_moment[:, 0 : B - 1, :],
+                in0=sum_exx[:, 0 : B - 1, :],
+                in1=inv_sum_e[:, 0 : B - 1, :],
+                op=ALU.mult,
+            )
+            nc.vector.tensor_tensor(out=v[:, :, 0, :], in0=sum_ex[:], in1=inv_sum_e[:], op=ALU.mult)
+            for ct, b in weighted_units:
+                exx = frames.tile([P, T], F32, tag="exx", bufs=2)
+                nc.vector.scalar_tensor_tensor(
+                    out=exx[:],
+                    in0=ex_tiles[(ct, b)][:],
+                    scalar=inv_sum_e[:, b, ct : ct + 1],
+                    in1=x_sb[:, b, ct, :],
+                    op0=ALU.mult,
+                    op1=ALU.mult,
+                    accum_out=second_moment[:, b, ct : ct + 1],
+                )
+                if ct == 0:
+                    nc.vector.tensor_tensor(
+                        out=squares[:, :, 0, :], in0=v[:, :, 0, :], in1=v[:, :, 0, :], op=ALU.mult
+                    )
             variance = small.tile([P, B, C_TILES], F32)
             nc.vector.tensor_tensor(
                 out=variance[:], in0=second_moment[:], in1=squares[:, :, 0, :], op=ALU.subtract

@@ -136,6 +136,9 @@ def tile_attentivestatspool_pb_k_kernel(tc, h, x, mask, w2, b2, g2, be2, out):
                 return [(i, b) for b in range(B) if ("h", b, g) in quantised]
             return [(ct, i) for ct in range(C_TILES) if ("w", ct, g) in quantised]
 
+        def load_x(b):
+            nc.sync.dma_start(out=x_sb[:, b, :, :], in_=x[b].rearrange("(ct p) t -> p ct t", p=P))
+
         def load(n):
             kind, i, first, passes = stream[n]
             k_rows = slice(first * K_PASS, (first + passes) * K_PASS)
@@ -150,10 +153,10 @@ def tile_attentivestatspool_pb_k_kernel(tc, h, x, mask, w2, b2, g2, be2, out):
                     in_=h[i, k_rows, :].rearrange("(g p j) t -> p g j t", p=P, j=PACK),
                 )
                 raw_tiles[n] = h_raw
-                if first + passes == PASSES:
-                    nc.sync.dma_start(
-                        out=x_sb[:, i, :, :], in_=x[i].rearrange("(ct p) t -> p ct t", p=P)
-                    )
+                if i > 0 and first == CHUNKS[0]:
+                    load_x(i - 1)
+                if i == B - 1 and first + passes == PASSES:
+                    load_x(i)
 
         def transpose(n):
             kind, i, first, passes = stream[n]

@@ -21,12 +21,11 @@ PACK = 4
 K_PASS = P * PACK
 PASSES = H // K_PASS
 C_TILES = C // P
-FIRST_CHUNKS = (2, 2, 4, 4, 4)
 CHUNKS = (4, 4, 4, 4)
 BANK = 512
 ROWS = 2 * C_TILES
 
-VECTOR_FRAMES = (160, 144, 104, 88)
+VECTOR_FRAMES = (160, 144, 112, 88)
 RUN = 4
 RAW_BUFS = 4
 MASKED = 1.0e30
@@ -110,7 +109,7 @@ def tile_attentivestatspool_pb_k_kernel(tc, h, x, mask, w2, b2, g2, be2, out):
             return [chunk for together in zip(*operands) for chunk in together]
 
         stream = in_turn(
-            chunks_of("w", 0, FIRST_CHUNKS), chunks_of("h", 0, FIRST_CHUNKS), chunks_of("w", 1, FIRST_CHUNKS)
+            chunks_of("w", 0, CHUNKS), chunks_of("h", 0, CHUNKS), chunks_of("w", 1, CHUNKS)
         )
         for i in range(1, B):
             if i + 1 < C_TILES:
@@ -310,8 +309,6 @@ def tile_attentivestatspool_pb_k_kernel(tc, h, x, mask, w2, b2, g2, be2, out):
                 n_loaded[0] += 1
                 if n_loaded[0] == n_chunks:
                     load_gain_and_bias()
-            if n + 1 < n_chunks:
-                transpose(n + 1)
             if n == 7:
                 spread_mask()
             to_weigh = take(weighted_units)
@@ -328,15 +325,17 @@ def tile_attentivestatspool_pb_k_kernel(tc, h, x, mask, w2, b2, g2, be2, out):
             for ct, b in to_negate:
                 find_maximum(ct, b)
             second_sums(to_weigh, ex_tiles)
-            if 1 <= n <= n_chunks:
+            if 1 <= n < n_chunks + 1:
                 quantise(n - 1)
             if n == 8:
                 use_mask()
-            if 2 <= n:
-                multiply(n - 2)
+            if 3 <= n:
+                multiply(n - 3)
+            if n + 1 < n_chunks:
+                transpose(n + 1)
 
         with tc.manual_schedule():
-            for n in range(-1, n_chunks + 2):
+            for n in range(-1, n_chunks + 3):
                 step(n)
             to_weigh = take(weighted_units)
             last = take(finished)

@@ -43,10 +43,10 @@ def tile_attentivestatspool_pb_k_kernel(tc, h, x, mask, w2, b2, g2, be2, out):
         psum = ctx.enter_context(tc.psum_pool(name="psum", bufs=8))
         small = ctx.enter_context(tc.tile_pool(name="small", bufs=1))
 
-        w_codes = keep.tile([P, C_TILES, PASSES, P], U32, align_bytes=64)
-        w_scales = keep.tile([P, C_TILES, PASSES, P], U8, align_bytes=64)
-        h_codes = keep.tile([P, B, PASSES, T], U32, align_bytes=64)
-        h_scales = keep.tile([P, B, PASSES, T], U8, align_bytes=64)
+        w_codes = keep.tile([P, C_TILES, PASSES, P], U32, align_bytes=256)
+        w_scales = keep.tile([P, C_TILES, PASSES, P], U8, align_bytes=256)
+        h_codes = keep.tile([P, B, PASSES, T], U32, align_bytes=256)
+        h_scales = keep.tile([P, B, PASSES, T], U8, align_bytes=256)
         x_sb = keep.tile([P, B, C_TILES, T], BF16)
         masked_add = keep.tile([P, B, T], F32)
         neg_max = keep.tile([P, B, C_TILES], F32)
@@ -113,7 +113,7 @@ def tile_attentivestatspool_pb_k_kernel(tc, h, x, mask, w2, b2, g2, be2, out):
         )
         for i in range(1, B):
             if i + 1 < C_TILES:
-                stream += in_turn(chunks_of("w", i + 1, CHUNKS), chunks_of("h", i, CHUNKS))
+                stream += in_turn(chunks_of("h", i, CHUNKS), chunks_of("w", i + 1, CHUNKS))
             else:
                 stream += chunks_of("h", i, CHUNKS)
         n_chunks = len(stream)
@@ -175,7 +175,7 @@ def tile_attentivestatspool_pb_k_kernel(tc, h, x, mask, w2, b2, g2, be2, out):
         def group(n):
             kind, i, first, passes = stream[n]
             if kind == "w":
-                w_grouped = grouped.tile([P, passes, P, PACK], BF16, tag="w_grouped", align_bytes=64)
+                w_grouped = grouped.tile([P, passes, P, PACK], BF16, tag="w_grouped", align_bytes=256)
                 grouped_words = w_grouped[:].bitcast(F32)
                 for pair, transposed in enumerate(transposed_banks[n]):
                     nc.scalar.copy(
@@ -184,7 +184,7 @@ def tile_attentivestatspool_pb_k_kernel(tc, h, x, mask, w2, b2, g2, be2, out):
                     )
                 grouped_tiles[n] = w_grouped
             else:
-                h_grouped = grouped.tile([P, passes, T, PACK], BF16, tag="h_grouped", align_bytes=64)
+                h_grouped = grouped.tile([P, passes, T, PACK], BF16, tag="h_grouped", align_bytes=256)
                 src = raw_tiles[n][:].rearrange("p g j (c r) -> p g c j r", r=RUN)
                 dst = h_grouped[:].rearrange("p g (c r) j -> p g c j r", r=RUN)
                 split = VECTOR_FRAMES[i] // RUN

@@ -38,7 +38,7 @@ def tile_attentivestatspool_pb_k_kernel(tc, h, x, mask, w2, b2, g2, be2, out):
     with ExitStack() as ctx:
         keep = ctx.enter_context(tc.tile_pool(name="keep", bufs=1))
         raw = ctx.enter_context(tc.tile_pool(name="raw", bufs=RAW_BUFS))
-        grouped = ctx.enter_context(tc.tile_pool(name="grouped", bufs=3))
+        grouped = ctx.enter_context(tc.tile_pool(name="grouped", bufs=1))
         frames = ctx.enter_context(tc.tile_pool(name="frames", bufs=3))
         psum = ctx.enter_context(tc.psum_pool(name="psum", bufs=8))
         small = ctx.enter_context(tc.tile_pool(name="small", bufs=1))
@@ -48,7 +48,7 @@ def tile_attentivestatspool_pb_k_kernel(tc, h, x, mask, w2, b2, g2, be2, out):
         h_codes = keep.tile([P, B, PASSES, T], U32, align_bytes=256)
         h_scales = keep.tile([P, B, PASSES, T], U8, align_bytes=256)
         x_sb = keep.tile([P, B, C_TILES, T], BF16)
-        masked_add = keep.tile([P, B, T], F32)
+        masked_add = keep.tile([P, B, T], BF16)
         neg_max = keep.tile([P, B, C_TILES], F32)
         sum_e = keep.tile([P, B, C_TILES], F32)
         sum_ex = keep.tile([P, B, C_TILES], F32)
@@ -175,7 +175,7 @@ def tile_attentivestatspool_pb_k_kernel(tc, h, x, mask, w2, b2, g2, be2, out):
         def group(n):
             kind, i, first, passes = stream[n]
             if kind == "w":
-                w_grouped = grouped.tile([P, passes, P, PACK], BF16, tag="w_grouped", align_bytes=256)
+                w_grouped = grouped.tile([P, passes, P, PACK], BF16, tag="w_grouped", bufs=3, align_bytes=256)
                 grouped_words = w_grouped[:].bitcast(F32)
                 for pair, transposed in enumerate(transposed_banks[n]):
                     nc.scalar.copy(
@@ -184,7 +184,9 @@ def tile_attentivestatspool_pb_k_kernel(tc, h, x, mask, w2, b2, g2, be2, out):
                     )
                 grouped_tiles[n] = w_grouped
             else:
-                h_grouped = grouped.tile([P, passes, T, PACK], BF16, tag="h_grouped", align_bytes=256)
+                h_grouped = grouped.tile(
+                    [P, passes, T, PACK], BF16, tag="h_grouped", bufs=2, align_bytes=256
+                )
                 src = raw_tiles[n][:].rearrange("p g j (c r) -> p g c j r", r=RUN)
                 dst = h_grouped[:].rearrange("p g (c r) j -> p g c j r", r=RUN)
                 split = VECTOR_FRAMES[i] // RUN
@@ -242,7 +244,7 @@ def tile_attentivestatspool_pb_k_kernel(tc, h, x, mask, w2, b2, g2, be2, out):
             negated_units.append((ct, b))
 
         def exponentials(ct, b):
-            e = frames.tile([P, T], F32, tag="e", bufs=4)
+            e = frames.tile([P, T], F32, tag="e", bufs=8)
             nc.scalar.activation(
                 out=e[:],
                 in_=negated_tiles[(ct, b)][:],
@@ -283,8 +285,33 @@ def tile_attentivestatspool_pb_k_kernel(tc, h, x, mask, w2, b2, g2, be2, out):
                     accum_out=sum_exx[:, b, ct : ct + 1],
                 )
 
-        def weighted_sums(units):
-            second_sums(units, first_sums(units))
+        def multiply_by_x(engine, out, values, unit):
+            ct, b = unit
+            engine.tensor_tensor(out=out, in0=values, in1=x_sb[:, b, ct, :], op=ALU.mult)
+
+        to_sum = []
+
+        def products_alone(units):
+            ex_tiles = {}
+            for unit in units:
+                ex = frames.tile([P, T], F32, tag="ex", bufs=4)
+                multiply_by_x(nc.vector, ex[:], e_tiles[unit][:], unit)
+                to_sum.append((ex[:], sum_ex, unit))
+                ex_tiles[unit] = ex
+            return ex_tiles
+
+        def second_products_alone(units, ex_tiles):
+            for unit in units:
+                exx = frames.tile([P, T], F32, tag="exx", bufs=2)
+                multiply_by_x(nc.vector, exx[:], ex_tiles[unit][:], unit)
+                to_sum.append((exx[:], sum_exx, unit))
+
+        def sum_on_scalar(values, sums, unit):
+            ct, b = unit
+            summed = frames.tile([P, T], F32, tag="summed", bufs=2)
+            nc.scalar.activation(
+                out=summed[:], in_=values, func=ACT.Copy, accum_out=sums[:, b, ct : ct + 1]
+            )
 
         def take(units):
             taken = units[:]
@@ -316,7 +343,7 @@ def tile_attentivestatspool_pb_k_kernel(tc, h, x, mask, w2, b2, g2, be2, out):
             to_negate = [finished.pop(0) for c in range(min(len(finished), 2))]
             for ct, b in to_negate:
                 negate(ct, b)
-            ex_tiles = first_sums(to_weigh)
+            ex_tiles = products_alone(to_weigh) if n == n_chunks else first_sums(to_weigh)
             for ct, b in to_exponentiate:
                 exponentials(ct, b)
             if 0 <= n < n_chunks:
@@ -324,7 +351,10 @@ def tile_attentivestatspool_pb_k_kernel(tc, h, x, mask, w2, b2, g2, be2, out):
                 n_wanted[stream[n][0]] += 1
             for ct, b in to_negate:
                 find_maximum(ct, b)
-            second_sums(to_weigh, ex_tiles)
+            if n == n_chunks:
+                second_products_alone(to_weigh, ex_tiles)
+            else:
+                second_sums(to_weigh, ex_tiles)
             if 1 <= n < n_chunks + 1:
                 quantise(n - 1)
             if n == 8:
@@ -335,22 +365,46 @@ def tile_attentivestatspool_pb_k_kernel(tc, h, x, mask, w2, b2, g2, be2, out):
                 transpose(n + 1)
 
         with tc.manual_schedule():
-            for n in range(-1, n_chunks + 3):
+            for n in range(-1, n_chunks + 1):
                 step(n)
-            to_weigh = take(weighted_units)
-            last = take(finished)
             for ct, b in take(negated_units):
                 exponentials(ct, b)
+            for values, sums, unit in to_sum:
+                sum_on_scalar(values, sums, unit)
+            multiply(n_chunks - 2)
+            multiply(n_chunks - 1)
+            early = take(weighted_units)
+            last = take(finished)
+            early_ex = frames.tile([P, len(early), T], F32, tag="early_ex", bufs=1)
+            marker = keep.tile([P, 1], U32)
+            nc.gpsimd.tensor_copy(out=marker[:], in_=h_codes[:, B - 1, PASSES - 1, 0:1])
+
+            def early_first(engine, i):
+                multiply_by_x(engine, early_ex[:, i, :], e_tiles[early[i]][:], early[i])
+
+            def early_second(i):
+                e = e_tiles[early[i]]
+                multiply_by_x(nc.vector, e[:], early_ex[:, i, :], early[i])
+                sum_on_scalar(e[:], sum_exx, early[i])
+
+            for i, engine in enumerate((nc.vector, nc.vector, nc.gpsimd, nc.gpsimd)):
+                early_first(engine, i)
+            for i in (0, 1):
+                sum_on_scalar(early_ex[:, i, :], sum_ex, early[i])
+            early_second(0)
             negate(*last[0])
-            weighted_sums(to_weigh)
-            to_weigh = take(weighted_units)
             for i, unit in enumerate(last):
                 if i + 1 < len(last):
                     negate(*last[i + 1])
-                elif to_weigh:
-                    weighted_sums(to_weigh)
                 find_maximum(*unit)
                 exponentials(*take(negated_units)[0])
+                if i in (1, 2):
+                    sum_on_scalar(early_ex[:, i + 1, :], sum_ex, early[i + 1])
+            last_ex = frames.tile([P, T], F32, tag="ex", bufs=4)
+            multiply_by_x(nc.gpsimd, last_ex[:], e_tiles[last[0]][:], last[0])
+            sum_on_scalar(last_ex[:], sum_ex, last[0])
+            for i in (1, 2, 3):
+                early_second(i)
 
             nc.scalar.activation(
                 out=table_warmer[:], in_=sum_e[:, B - 1, C_TILES - 1 : C_TILES], func=ACT.Sqrt
@@ -359,15 +413,10 @@ def tile_attentivestatspool_pb_k_kernel(tc, h, x, mask, w2, b2, g2, be2, out):
             squares = small.tile([P, B, 2, C_TILES], F32)
             inv_sum_e = small.tile([P, B, C_TILES], F32)
             second_moment = small.tile([P, B, C_TILES], F32)
-            ex_tiles = first_sums(weighted_units[:-1])
+            ex_tiles = {last[0]: last_ex}
+            ex_tiles.update(first_sums(weighted_units[1:-1]))
             nc.vector.reciprocal(out=inv_sum_e[:], in_=sum_e[:])
             ex_tiles.update(first_sums(weighted_units[-1:]))
-            nc.vector.tensor_tensor(
-                out=second_moment[:, 0 : B - 1, :],
-                in0=sum_exx[:, 0 : B - 1, :],
-                in1=inv_sum_e[:, 0 : B - 1, :],
-                op=ALU.mult,
-            )
             nc.vector.tensor_tensor(out=v[:, :, 0, :], in0=sum_ex[:], in1=inv_sum_e[:], op=ALU.mult)
             for ct, b in weighted_units:
                 exx = frames.tile([P, T], F32, tag="exx", bufs=2)
@@ -383,6 +432,13 @@ def tile_attentivestatspool_pb_k_kernel(tc, h, x, mask, w2, b2, g2, be2, out):
                 if ct == 0:
                     nc.vector.tensor_tensor(
                         out=squares[:, :, 0, :], in0=v[:, :, 0, :], in1=v[:, :, 0, :], op=ALU.mult
+                    )
+                if ct == C_TILES - 2:
+                    nc.vector.tensor_tensor(
+                        out=second_moment[:, 0 : B - 1, :],
+                        in0=sum_exx[:, 0 : B - 1, :],
+                        in1=inv_sum_e[:, 0 : B - 1, :],
+                        op=ALU.mult,
                     )
             variance = small.tile([P, B, C_TILES], F32)
             nc.vector.tensor_tensor(

@@ -28,6 +28,7 @@ ROWS = 2 * C_TILES
 VECTOR_FRAMES = (160, 144, 112, 88)
 RUN = 4
 RAW_BUFS = 4
+GPSIMD_FRAMES = 32
 MASKED = 1.0e30
 
 FLOPS = 2 * B * C * H * T
@@ -172,7 +173,13 @@ def tile_attentivestatspool_pb_k_kernel(tc, h, x, mask, w2, b2, g2, be2, out):
                         )
                 transposed_banks[n].append(transposed)
 
-        def group(n):
+        def gpsimd_waits_for_quantised(n):
+            kind, i, first, passes = stream[n]
+            codes = w_codes if kind == "w" else h_codes
+            marker = small.tile([P, 1], U32, tag="marker", bufs=2)
+            nc.gpsimd.tensor_copy(out=marker[:], in_=codes[:, i, first + passes - 1, 0:1])
+
+        def group(n, with_gpsimd):
             kind, i, first, passes = stream[n]
             if kind == "w":
                 w_grouped = grouped.tile([P, passes, P, PACK], BF16, tag="w_grouped", bufs=3, align_bytes=256)
@@ -190,7 +197,21 @@ def tile_attentivestatspool_pb_k_kernel(tc, h, x, mask, w2, b2, g2, be2, out):
                 src = raw_tiles[n][:].rearrange("p g j (c r) -> p g c j r", r=RUN)
                 dst = h_grouped[:].rearrange("p g (c r) j -> p g c j r", r=RUN)
                 split = VECTOR_FRAMES[i] // RUN
-                nc.vector.tensor_copy(out=dst[:, :, 0:split], in_=src[:, :, 0:split])
+                on_gpsimd = 0
+                if with_gpsimd:
+                    on_gpsimd = GPSIMD_FRAMES // RUN
+                    gpsimd_waits_for_quantised(n - 2)
+                    nc.gpsimd.tensor_scalar(
+                        out=h_grouped[:, :, 0:GPSIMD_FRAMES, :],
+                        in0=raw_tiles[n][:, :, :, 0:GPSIMD_FRAMES].rearrange("p g j t -> p g t j"),
+                        scalar1=1.0,
+                        scalar2=1.0,
+                        op0=ALU.mult,
+                        op1=ALU.mult,
+                    )
+                nc.vector.tensor_copy(
+                    out=dst[:, :, on_gpsimd:split], in_=src[:, :, on_gpsimd:split]
+                )
                 for g in range(passes):
                     nc.scalar.copy(out=dst[:, g, split:], in_=src[:, g, split:])
                 grouped_tiles[n] = h_grouped
@@ -343,14 +364,19 @@ def tile_attentivestatspool_pb_k_kernel(tc, h, x, mask, w2, b2, g2, be2, out):
             to_negate = [finished.pop(0) for c in range(min(len(finished), 2))]
             for ct, b in to_negate:
                 negate(ct, b)
+            with_gpsimd = len(to_negate) == 2 and n < n_chunks and stream[n][0] == "h"
+            if with_gpsimd:
+                for ct, b in to_negate:
+                    find_maximum(ct, b)
             ex_tiles = products_alone(to_weigh) if n == n_chunks else first_sums(to_weigh)
             for ct, b in to_exponentiate:
                 exponentials(ct, b)
             if 0 <= n < n_chunks:
-                group(n)
+                group(n, with_gpsimd)
                 n_wanted[stream[n][0]] += 1
-            for ct, b in to_negate:
-                find_maximum(ct, b)
+            if not with_gpsimd:
+                for ct, b in to_negate:
+                    find_maximum(ct, b)
             if n == n_chunks:
                 second_products_alone(to_weigh, ex_tiles)
             else:
@@ -376,8 +402,7 @@ def tile_attentivestatspool_pb_k_kernel(tc, h, x, mask, w2, b2, g2, be2, out):
             early = take(weighted_units)
             last = take(finished)
             early_ex = frames.tile([P, len(early), T], F32, tag="early_ex", bufs=1)
-            marker = keep.tile([P, 1], U32)
-            nc.gpsimd.tensor_copy(out=marker[:], in_=h_codes[:, B - 1, PASSES - 1, 0:1])
+            gpsimd_waits_for_quantised(n_chunks - 1)
 
             def early_first(engine, i):
                 multiply_by_x(engine, early_ex[:, i, :], e_tiles[early[i]][:], early[i])

from contextlib import ExitStack

import concourse.mybir as mybir
from concourse.masks import make_identity

F32 = mybir.dt.float32
BF16 = mybir.dt.bfloat16
U32 = mybir.dt.uint32
U8 = mybir.dt.uint8
FP8X4 = mybir.dt.float8_e4m3fn_x4
ALU = mybir.AluOpType
ACT = mybir.ActivationFunctionType
AXIS = mybir.AxisListType

B, C, T, H = 4, 512, 256, 8192
EPS_LN = 1e-5
EPS_STD = 1e-5

P = 128
PACK = 4
K_PASS = P * PACK
PASSES = H // K_PASS
C_TILES = C // P
CHUNKS = (4, 4, 4, 4)
BANK = 512
ROWS = 2 * C_TILES

VECTOR_FRAMES = (160, 144, 112, 88)
RUN = 4
RAW_BUFS = 4
GPSIMD_FRAMES = 32
MASKED = 1.0e30

FLOPS = 2 * B * C * H * T


def tile_attentivestatspool_pb_k_kernel(tc, h, x, mask, w2, b2, g2, be2, out):
    nc = tc.nc
    with ExitStack() as ctx:
        keep = ctx.enter_context(tc.tile_pool(name="keep", bufs=1))
        raw = ctx.enter_context(tc.tile_pool(name="raw", bufs=RAW_BUFS))
        grouped = ctx.enter_context(tc.tile_pool(name="grouped", bufs=1))
        frames = ctx.enter_context(tc.tile_pool(name="frames", bufs=3))
        psum = ctx.enter_context(tc.psum_pool(name="psum", bufs=8))
        small = ctx.enter_context(tc.tile_pool(name="small", bufs=1))

        w_codes = keep.tile([P, C_TILES, PASSES, P], U32, align_bytes=256)
        w_scales = keep.tile([P, C_TILES, PASSES, P], U8, align_bytes=256)
        h_codes = keep.tile([P, B, PASSES, T], U32, align_bytes=256)
        h_scales = keep.tile([P, B, PASSES, T], U8, align_bytes=256)
        x_sb = keep.tile([P, B, C_TILES, T], BF16)
        masked_add = keep.tile([P, B, T], BF16)
        neg_max = keep.tile([P, B, C_TILES], F32)
        sum_e = keep.tile([P, B, C_TILES], F32)
        sum_ex = keep.tile([P, B, C_TILES], F32)
        sum_exx = keep.tile([P, B, C_TILES], F32)

        identity = keep.tile([P, P], F32)
        make_identity(nc, identity[:])
        mask_rows = keep.tile([P, B * T], BF16)
        nc.vector.memset(mask_rows[:], 0.0)
        nc.scalar.dma_start(out=mask_rows[0:1, :], in_=mask.rearrange("b o t -> o (b t)"))
        ones = keep.tile([P, P], BF16)
        nc.vector.memset(ones[:], 1.0)
        one_column = keep.tile([P, 1], F32)
        nc.vector.memset(one_column[:], 1.0)
        averager = keep.tile([P, 1], F32)
        nc.gpsimd.memset(averager[:], 1.0 / (2 * C))
        eps_column = keep.tile([P, 1], F32)
        nc.gpsimd.memset(eps_column[:], EPS_LN)
        v_wide = keep.tile([P, P], F32)
        nc.gpsimd.memset(v_wide[:], 0.0)
        sums_wide = keep.tile([P, P], F32)
        nc.gpsimd.memset(sums_wide[:], 0.0)
        squares_wide = keep.tile([P, P], F32)
        nc.gpsimd.memset(squares_wide[:], 0.0)

        table_warmer = keep.tile([P, 1], F32)
        nc.scalar.activation(out=table_warmer[:], in_=one_column[:], func=ACT.Exp)

        masked_add_flat = masked_add[:].rearrange("p b t -> p (b t)")

        mask_banks = []

        def spread_mask():
            for half in range(B * T // BANK):
                cols = slice(half * BANK, (half + 1) * BANK)
                mask_everywhere = psum.tile([P, BANK], F32, tag="bank")
                nc.tensor.matmul(
                    out=mask_everywhere[:], lhsT=ones[:], rhs=mask_rows[:, cols], start=True, stop=True
                )
                mask_banks.append(mask_everywhere)

        def use_mask():
            for half, mask_everywhere in enumerate(mask_banks):
                cols = slice(half * BANK, (half + 1) * BANK)
                nc.vector.tensor_scalar(
                    out=masked_add_flat[:, cols],
                    in0=mask_everywhere[:],
                    scalar1=0.0,
                    scalar2=MASKED,
                    op0=ALU.is_equal,
                    op1=ALU.mult,
                )

        def chunks_of(kind, i, sizes):
            return [(kind, i, sum(sizes[:c]), sizes[c]) for c in range(len(sizes))]

        def in_turn(*operands):
            return [chunk for together in zip(*operands) for chunk in together]

        stream = in_turn(
            chunks_of("w", 0, CHUNKS), chunks_of("h", 0, CHUNKS), chunks_of("w", 1, CHUNKS)
        )
        for i in range(1, B):
            if i + 1 < C_TILES:
                stream += in_turn(chunks_of("h", i, CHUNKS), chunks_of("w", i + 1, CHUNKS))
            else:
                stream += chunks_of("h", i, CHUNKS)
        n_chunks = len(stream)

        raw_tiles = {}
        transposed_banks = {}
        grouped_tiles = {}
        logits = {}
        negated_tiles = {}
        e_tiles = {}
        finished = []
        negated_units = []
        weighted_units = []

        quantised = set()

        def units_of(kind, i, g):
            if kind == "w":
                return [(i, b) for b in range(B) if ("h", b, g) in quantised]
            return [(ct, i) for ct in range(C_TILES) if ("w", ct, g) in quantised]

        def load_x(b):
            nc.sync.dma_start(out=x_sb[:, b, :, :], in_=x[b].rearrange("(ct p) t -> p ct t", p=P))

        def load(n):
            kind, i, first, passes = stream[n]
            k_rows = slice(first * K_PASS, (first + passes) * K_PASS)
            if kind == "w":
                w_raw = raw.tile([P, passes * K_PASS], BF16, tag="w_raw")
                nc.sync.dma_start(out=w_raw[:], in_=w2[i * P : (i + 1) * P, k_rows])
                raw_tiles[n] = w_raw
            else:
                h_raw = raw.tile([P, passes, PACK, T], BF16, tag="h_raw")
                nc.sync.dma_start(
                    out=h_raw[:],
                    in_=h[i, k_rows, :].rearrange("(g p j) t -> p g j t", p=P, j=PACK),
                )
                raw_tiles[n] = h_raw
                if i > 0 and first == CHUNKS[0]:
                    load_x(i - 1)
                if i == B - 1 and first + passes == PASSES:
                    load_x(i)

        def transpose(n):
            kind, i, first, passes = stream[n]
            if kind == "h":
                return
            words = raw_tiles[n][:].bitcast(F32).rearrange("c (g q u) -> c g u q", g=passes, u=2)
            transposed_banks[n] = []
            for pair in range(passes // 2):
                transposed = psum.tile([P, 2, 2, P], F32, tag="bank")
                for g in range(2):
                    for u in range(2):
                        nc.tensor.transpose(
                            transposed[:, g, u, :], words[:, 2 * pair + g, u, :], identity[:]
                        )
                transposed_banks[n].append(transposed)

        def gpsimd_waits_for_quantised(n):
            kind, i, first, passes = stream[n]
            codes = w_codes if kind == "w" else h_codes
            marker = small.tile([P, 1], U32, tag="marker", bufs=2)
            nc.gpsimd.tensor_copy(out=marker[:], in_=codes[:, i, first + passes - 1, 0:1])

        def group(n, with_gpsimd):
            kind, i, first, passes = stream[n]
            if kind == "w":
                w_grouped = grouped.tile([P, passes, P, PACK], BF16, tag="w_grouped", bufs=3, align_bytes=256)
                grouped_words = w_grouped[:].bitcast(F32)
                for pair, transposed in enumerate(transposed_banks[n]):
                    nc.scalar.copy(
                        out=grouped_words[:, 2 * pair : 2 * pair + 2, :, :],
                        in_=transposed[:].rearrange("q g u c -> q g c u"),
                    )
                grouped_tiles[n] = w_grouped
            else:
                h_grouped = grouped.tile(
                    [P, passes, T, PACK], BF16, tag="h_grouped", bufs=2, align_bytes=256
                )
                src = raw_tiles[n][:].rearrange("p g j (c r) -> p g c j r", r=RUN)
                dst = h_grouped[:].rearrange("p g (c r) j -> p g c j r", r=RUN)
                split = VECTOR_FRAMES[i] // RUN
                on_gpsimd = 0
                if with_gpsimd:
                    on_gpsimd = GPSIMD_FRAMES // RUN
                    gpsimd_waits_for_quantised(n - 2)
                    nc.gpsimd.tensor_scalar(
                        out=h_grouped[:, :, 0:GPSIMD_FRAMES, :],
                        in0=raw_tiles[n][:, :, :, 0:GPSIMD_FRAMES].rearrange("p g j t -> p g t j"),
                        scalar1=1.0,
                        scalar2=1.0,
                        op0=ALU.mult,
                        op1=ALU.mult,
                    )
                nc.vector.tensor_copy(
                    out=dst[:, :, on_gpsimd:split], in_=src[:, :, on_gpsimd:split]
                )
                for g in range(passes):
                    nc.scalar.copy(out=dst[:, g, split:], in_=src[:, g, split:])
                grouped_tiles[n] = h_grouped

        def quantise(n):
            kind, i, first, n_passes = stream[n]
            passes = slice(first, first + n_passes)
            codes, scales = (w_codes, w_scales) if kind == "w" else (h_codes, h_scales)
            nc.vector.quantize_mx(
                out=codes[:, i, passes, :].rearrange("p g n -> p (g n)").bitcast(FP8X4),
                scales=scales[:, i, passes, :].rearrange("p g n -> p (g n)"),
                in_=grouped_tiles[n][:].rearrange("p g n j -> p (g n j)"),
            )

        def multiply(n):
            kind, i, first, passes = stream[n]
            for g in range(first, first + passes):
                quantised.add((kind, i, g))
            for ct, b in units_of(kind, i, first):
                if first == 0:
                    logits[(ct, b)] = psum.tile([P, BANK], F32, tag="bank", name="unit_logits")
                for g in range(first, first + passes):
                    nc.tensor.matmul_mx(
                        out=logits[(ct, b)][:, 0:T],
                        lhsT=w_codes[:, ct, g, :].bitcast(FP8X4),
                        lhsT_scale=w_scales[:, ct, g, :],
                        rhs=h_codes[:, b, g, :].bitcast(FP8X4),
                        rhs_scale=h_scales[:, b, g, :],
                        start=(g == 0),
                        stop=(g == PASSES - 1),
                    )
                if first + passes == PASSES:
                    finished.append((ct, b))

        def negate(ct, b):
            negated = frames.tile([P, T], F32, tag="negated", bufs=4)
            nc.vector.scalar_tensor_tensor(
                out=negated[:],
                in0=logits[(ct, b)][:, 0:T],
                scalar=-1.0,
                in1=masked_add[:, b, :],
                op0=ALU.mult,
                op1=ALU.add,
            )
            negated_tiles[(ct, b)] = negated

        def find_maximum(ct, b):
            nc.vector.tensor_reduce(
                out=neg_max[:, b, ct : ct + 1], in_=negated_tiles[(ct, b)][:], axis=AXIS.X, op=ALU.min
            )
            negated_units.append((ct, b))

        def exponentials(ct, b):
            e = frames.tile([P, T], F32, tag="e", bufs=8)
            nc.scalar.activation(
                out=e[:],
                in_=negated_tiles[(ct, b)][:],
                func=ACT.Exp,
                scale=-1.0,
                bias=neg_max[:, b, ct : ct + 1],
                accum_out=sum_e[:, b, ct : ct + 1],
            )
            e_tiles[(ct, b)] = e
            weighted_units.append((ct, b))

        def first_sums(units):
            ex_tiles = {}
            for ct, b in units:
                ex = frames.tile([P, T], F32, tag="ex", bufs=4)
                nc.vector.scalar_tensor_tensor(
                    out=ex[:],
                    in0=e_tiles[(ct, b)][:],
                    scalar=1.0,
                    in1=x_sb[:, b, ct, :],
                    op0=ALU.mult,
                    op1=ALU.mult,
                    accum_out=sum_ex[:, b, ct : ct + 1],
                )
                ex_tiles[(ct, b)] = ex
            return ex_tiles

        def second_sums(units, ex_tiles):
            for ct, b in units:
                exx = frames.tile([P, T], F32, tag="exx", bufs=2)
                nc.vector.scalar_tensor_tensor(
                    out=exx[:],
                    in0=ex_tiles[(ct, b)][:],
                    scalar=1.0,
                    in1=x_sb[:, b, ct, :],
                    op0=ALU.mult,
                    op1=ALU.mult,
                    accum_out=sum_exx[:, b, ct : ct + 1],
                )

        def multiply_by_x(engine, out, values, unit):
            ct, b = unit
            engine.tensor_tensor(out=out, in0=values, in1=x_sb[:, b, ct, :], op=ALU.mult)

        to_sum = []

        def products_alone(units):
            ex_tiles = {}
            for unit in units:
                ex = frames.tile([P, T], F32, tag="ex", bufs=4)
                multiply_by_x(nc.vector, ex[:], e_tiles[unit][:], unit)
                to_sum.append((ex[:], sum_ex, unit))
                ex_tiles[unit] = ex
            return ex_tiles

        def second_products_alone(units, ex_tiles):
            for unit in units:
                exx = frames.tile([P, T], F32, tag="exx", bufs=2)
                multiply_by_x(nc.vector, exx[:], ex_tiles[unit][:], unit)
                to_sum.append((exx[:], sum_exx, unit))

        def sum_on_scalar(values, sums, unit):
            ct, b = unit
            summed = frames.tile([P, T], F32, tag="summed", bufs=2)
            nc.scalar.activation(
                out=summed[:], in_=values, func=ACT.Copy, accum_out=sums[:, b, ct : ct + 1]
            )

        def take(units):
            taken = units[:]
            units.clear()
            return taken

        gain_rows = keep.tile([B * ROWS, P], BF16)
        bias_rows = keep.tile([B * ROWS, P], BF16)

        def load_gain_and_bias():
            for b in range(B):
                rows = slice(b * ROWS, (b + 1) * ROWS)
                nc.sync.dma_start(out=gain_rows[rows, :], in_=g2.rearrange("(r p) -> r p", p=P))
                nc.sync.dma_start(out=bias_rows[rows, :], in_=be2.rearrange("(r p) -> r p", p=P))

        n_loaded = [0]
        n_wanted = {"w": RAW_BUFS, "h": RAW_BUFS}
        def step(n):
            while n_loaded[0] < n_chunks and n_wanted[stream[n_loaded[0]][0]] > 0:
                n_wanted[stream[n_loaded[0]][0]] -= 1
                load(n_loaded[0])
                n_loaded[0] += 1
                if n_loaded[0] == n_chunks:
                    load_gain_and_bias()
            if n == 7:
                spread_mask()
            to_weigh = take(weighted_units)
            to_exponentiate = take(negated_units)
            to_negate = [finished.pop(0) for c in range(min(len(finished), 2))]
            for ct, b in to_negate:
                negate(ct, b)
            with_gpsimd = len(to_negate) == 2 and n < n_chunks and stream[n][0] == "h"
            if with_gpsimd:
                for ct, b in to_negate:
                    find_maximum(ct, b)
            ex_tiles = products_alone(to_weigh) if n == n_chunks else first_sums(to_weigh)
            for ct, b in to_exponentiate:
                exponentials(ct, b)
            if 0 <= n < n_chunks:
                group(n, with_gpsimd)
                n_wanted[stream[n][0]] += 1
            if not with_gpsimd:
                for ct, b in to_negate:
                    find_maximum(ct, b)
            if n == n_chunks:
                second_products_alone(to_weigh, ex_tiles)
            else:
                second_sums(to_weigh, ex_tiles)
            if 1 <= n < n_chunks + 1:
                quantise(n - 1)
            if n == 8:
                use_mask()
            if 3 <= n:
                multiply(n - 3)
            if n + 1 < n_chunks:
                transpose(n + 1)

        with tc.manual_schedule():
            for n in range(-1, n_chunks + 1):
                step(n)
            for ct, b in take(negated_units):
                exponentials(ct, b)
            for values, sums, unit in to_sum:
                sum_on_scalar(values, sums, unit)
            multiply(n_chunks - 2)
            multiply(n_chunks - 1)
            early = take(weighted_units)
            last = take(finished)
            early_ex = frames.tile([P, len(early), T], F32, tag="early_ex", bufs=1)
            gpsimd_waits_for_quantised(n_chunks - 1)

            def early_first(engine, i):
                multiply_by_x(engine, early_ex[:, i, :], e_tiles[early[i]][:], early[i])

            def early_second(i):
                e = e_tiles[early[i]]
                multiply_by_x(nc.vector, e[:], early_ex[:, i, :], early[i])
                sum_on_scalar(e[:], sum_exx, early[i])

            for i, engine in enumerate((nc.vector, nc.vector, nc.gpsimd, nc.gpsimd)):
                early_first(engine, i)
            for i in (0, 1):
                sum_on_scalar(early_ex[:, i, :], sum_ex, early[i])
            early_second(0)
            negate(*last[0])
            for i, unit in enumerate(last):
                if i + 1 < len(last):
                    negate(*last[i + 1])
                find_maximum(*unit)
                exponentials(*take(negated_units)[0])
                if i in (1, 2):
                    sum_on_scalar(early_ex[:, i + 1, :], sum_ex, early[i + 1])
            last_ex = frames.tile([P, T], F32, tag="ex", bufs=4)
            multiply_by_x(nc.gpsimd, last_ex[:], e_tiles[last[0]][:], last[0])
            sum_on_scalar(last_ex[:], sum_ex, last[0])
            for i in (1, 2, 3):
                early_second(i)

            nc.scalar.activation(
                out=table_warmer[:], in_=sum_e[:, B - 1, C_TILES - 1 : C_TILES], func=ACT.Sqrt
            )
            v = v_wide[:, 0 : B * ROWS].rearrange("p (b s ct) -> p b s ct", b=B, s=2)
            squares = small.tile([P, B, 2, C_TILES], F32)
            inv_sum_e = small.tile([P, B, C_TILES], F32)
            second_moment = small.tile([P, B, C_TILES], F32)
            ex_tiles = {last[0]: last_ex}
            ex_tiles.update(first_sums(weighted_units[1:-1]))
            nc.vector.reciprocal(out=inv_sum_e[:], in_=sum_e[:])
            ex_tiles.update(first_sums(weighted_units[-1:]))
            nc.vector.tensor_tensor(out=v[:, :, 0, :], in0=sum_ex[:], in1=inv_sum_e[:], op=ALU.mult)
            for ct, b in weighted_units:
                exx = frames.tile([P, T], F32, tag="exx", bufs=2)
                nc.vector.scalar_tensor_tensor(
                    out=exx[:],
                    in0=ex_tiles[(ct, b)][:],
                    scalar=inv_sum_e[:, b, ct : ct + 1],
                    in1=x_sb[:, b, ct, :],
                    op0=ALU.mult,
                    op1=ALU.mult,
                    accum_out=second_moment[:, b, ct : ct + 1],
                )
                if ct == 0:
                    nc.vector.tensor_tensor(
                        out=squares[:, :, 0, :], in0=v[:, :, 0, :], in1=v[:, :, 0, :], op=ALU.mult
                    )
                if ct == C_TILES - 2:
                    nc.vector.tensor_tensor(
                        out=second_moment[:, 0 : B - 1, :],
                        in0=sum_exx[:, 0 : B - 1, :],
                        in1=inv_sum_e[:, 0 : B - 1, :],
                        op=ALU.mult,
                    )
            variance = small.tile([P, B, C_TILES], F32)
            nc.vector.tensor_tensor(
                out=variance[:], in0=second_moment[:], in1=squares[:, :, 0, :], op=ALU.subtract
            )
            nc.vector.tensor_scalar_max(out=squares[:, :, 1, :], in0=variance[:], scalar1=EPS_STD)
            nc.scalar.sqrt(out=v[:, :, 1, :], in_=squares[:, :, 1, :])

            def averages(wide, values, name):
                eight = values.rearrange("p b s ct -> p b (s ct)").unsqueeze(2)
                nc.vector.tensor_reduce(
                    out=wide[:, 0 : B * ROWS].rearrange("p (b r) -> p b r", b=B),
                    in_=eight.to_broadcast([P, B, ROWS, ROWS]),
                    axis=AXIS.X,
                    op=ALU.add,
                )
                average_bank = psum.tile([P, BANK], F32, tag="bank", name=name)
                nc.tensor.matmul(
                    out=average_bank[:, 0:1], lhsT=wide[:], rhs=averager[:], start=True, stop=True
                )
                return average_bank[0 : B * ROWS, 0:1]

            mean_square = averages(squares_wide, squares[:], "mean_square_bank")
            v_rows = psum.tile([P, BANK], F32, tag="bank")
            nc.tensor.transpose(v_rows[:, 0:P], v_wide[:], identity[:])
            mu = averages(sums_wide, v, "mu_bank")
            negated_variance = small.tile([B * ROWS, 1], F32)
            nc.vector.tensor_scalar(
                out=negated_variance[:],
                in0=mu,
                scalar1=mu,
                scalar2=mean_square,
                op0=ALU.mult,
                op1=ALU.subtract,
            )
            ln_deviation = small.tile([B * ROWS, 1], F32)
            nc.scalar.activation(
                out=ln_deviation[:],
                in_=negated_variance[:],
                func=ACT.Sqrt,
                scale=-1.0,
                bias=eps_column[0 : B * ROWS, :],
            )
            scaled = small.tile([B * ROWS, P], F32)
            nc.vector.scalar_tensor_tensor(
                out=scaled[:],
                in0=v_rows[0 : B * ROWS, 0:P],
                scalar=mu,
                in1=gain_rows[:],
                op0=ALU.subtract,
                op1=ALU.mult,
            )
            inv_deviation = small.tile([B * ROWS, 1], F32)
            nc.vector.reciprocal(out=inv_deviation[:], in_=ln_deviation[:])
            result = small.tile([B * ROWS, P], F32)
            nc.vector.scalar_tensor_tensor(
                out=result[:],
                in0=scaled[:],
                scalar=inv_deviation[:],
                in1=bias_rows[:],
                op0=ALU.mult,
                op1=ALU.add,
            )
            nc.sync.dma_start(out=out.rearrange("b (r p) o -> (b r) (p o)", p=P), in_=result[:])
